import numpy as np
import ml_dtypes


def mxq(x, axis, fmt="e4m3"):
    dtype, down = {"e4m3": (ml_dtypes.float8_e4m3fn, 7), "e5m2": (ml_dtypes.float8_e5m2, 14)}[fmt]
    v = np.moveaxis(np.asarray(x, np.float32).astype(ml_dtypes.bfloat16).astype(np.float64), axis, -1)
    blocks = v.reshape(v.shape[:-1] + (-1, 32))
    amax = np.abs(blocks).max(-1, keepdims=True)
    byte = np.maximum(np.where(amax > 0, np.frexp(amax)[1] - 1 + 127, 0) - down, 1)
    scale = np.exp2(byte - 127.0)
    codes = (blocks / scale).astype(np.float32).astype(dtype).astype(np.float64)
    return np.moveaxis((codes * scale).reshape(v.shape), -1, axis)


WIDE = False


def mx_kscale(k):
    if not WIDE:
        return np.ones(k)
    levels = np.array([10, -10, 5, -5, 0])
    if k % 512:
        return np.exp2(np.random.permutation(np.resize(levels, k // 32))).repeat(32)
    a = np.empty((k // 512, 16))
    for p in range(k // 512):
        a[p, :8] = np.random.permutation(np.resize(levels, 8))
        for g in range(8):
            far = levels[np.abs(levels - a[p, g]) >= 10]
            a[p, g + 8] = far[np.random.randint(len(far))]
    return np.exp2(a.ravel()).repeat(32)


BF16 = ml_dtypes.bfloat16


def bf(x):
    return np.asarray(x, np.float32).astype(BF16)


def f64(x):
    return np.asarray(x).astype(np.float64)


B, D_IN, D_HID, D_OUT, LAT = 8192, 192, 512, 256, 16
BN_EPS = 1e-5
L2_EPS = 1e-12


def setup_inputs():
    t = mx_kscale(D_HID)
    col_sd = np.exp(0.4 * np.random.standard_normal(D_HID))
    col_mean = 0.5 * np.random.standard_normal(D_HID)
    return {
        "y_lin": bf(np.random.standard_normal((B, D_HID)) * col_sd + col_mean),
        "gamma": bf((1.0 + 0.2 * np.random.standard_normal(D_HID)) * t),
        "beta": bf(0.3 * np.random.standard_normal(D_HID) * t),
        "W2": bf(np.random.standard_normal((D_OUT, D_HID)) / np.sqrt(D_HID) / t[None, :]),
        "b2": bf(0.2 * np.random.standard_normal(D_OUT)),
    }


def reference(y_lin, gamma, beta, W2, b2):
    y = f64(y_lin)
    mean = np.mean(y, axis=0)
    var = np.mean((y - mean) ** 2, axis=0)
    y = (y - mean) * (1.0 / np.sqrt(var + BN_EPS)) * f64(gamma) + f64(beta)
    a = np.maximum(y, 0.0)
    p = (mxq(a, 1, "e4m3") @ mxq(f64(W2), 1, "e4m3").T) + f64(b2)
    n = np.sqrt(np.sum(p * p, axis=1, keepdims=True))
    return p / np.maximum(n, L2_EPS)

@@ -1,0 +1,343 @@
+from contextlib import ExitStack
+
+import concourse.mybir as mybir
+from concourse.masks import make_identity
+
+FLOPS = 2 * 8192 * 512 * 256
+
+FP8X4 = mybir.dt.float8_e4m3fn_x4
+BF16 = mybir.dt.bfloat16
+F32 = mybir.dt.float32
+U32 = mybir.dt.uint32
+U8 = mybir.dt.uint8
+ALU = mybir.AluOpType
+ACT = mybir.ActivationFunctionType
+AX = mybir.AxisListType
+
+P = 128
+B = 8192
+K = 512
+O = 256
+T = K // P
+G = B // P
+UNIT = 4
+NU = G // UNIT
+UC = UNIT * P
+SP = 2
+SUMQ = 4
+BN_EPS = 1e-5
+L2_EPS = 1e-12
+LOAD_BOUNDS = [0, 4, 8, 16, 24, 32, 40, 48, 56, 64]
+CHUNKS = [8, 8, 8, 8, 8, 8, 8, 4, 2, 2]
+CMAX = 8
+
+
+def tile_simclr_pa_t_kernel(tc, y_lin, gamma, beta, W2, b2, out):
+    nc = tc.nc
+    yv = y_lin.rearrange("(p g) k -> p g k", g=G)
+    ov = out.rearrange("(p g) o -> p g o", g=G)
+    with ExitStack() as ctx:
+        ctx.enter_context(tc.manual_schedule())
+        const = ctx.enter_context(tc.tile_pool(name="const", bufs=1))
+        Y = const.tile([P, G, K], BF16, name="Y")
+        one1 = const.tile([P, 1], F32, name="one1")
+        warm = const.tile([P, 1], F32, name="warm")
+        eps = const.tile([P, 1], F32, name="eps")
+        tiny = const.tile([P, 1], F32, name="tiny")
+        ident = const.tile([P, P], BF16, name="ident")
+        ones = const.tile([P, P], BF16, name="ones")
+        gb = const.tile([P, 2, 16], BF16, name="gb")
+        gbT = const.tile([P, 2 * T], F32, name="gbT")
+        b2z = const.tile([P, O], BF16, name="b2z")
+        b2b = const.tile([P, 2, O], F32, name="b2b")
+        w_sb = const.tile([P, 2, K], BF16, name="w_sb")
+        wt_sb = const.tile([P, T, O], BF16, name="wt_sb")
+        wg = const.tile([P, O, T], BF16, name="wg", align_bytes=64)
+        w_codes = const.tile([P, O], U32, name="w_codes", align_bytes=64)
+        w_scales = const.tile([P, O], U8, name="w_scales", align_bytes=64)
+        negm0 = const.tile([P, SP], F32, name="negm0")
+        sq = const.tile([P, SP * NU], F32, name="sq")
+        st = const.tile([P, T - SP, NU, 6], F32, name="st")
+        mv = const.tile([P, T, 2], F32, name="mv")
+        sxs = const.tile([P, SP], F32, name="sxs")
+        sqs = const.tile([P, SP], F32, name="sqs")
+        dm = const.tile([P, SP], F32, name="dm")
+        dm2 = const.tile([P, SP], F32, name="dm2")
+        nmg = const.tile([P, T], F32, name="nmg")
+        std = const.tile([P, T], F32, name="std")
+        rstd = const.tile([P, T], F32, name="rstd")
+        sc = const.tile([P, T], F32, name="sc")
+        sh = const.tile([P, T], F32, name="sh")
+
+        nc.vector.memset(b2z[:], 0.0)
+        nc.scalar.dma_start(out=gb[:, 0, 0:T], in_=gamma.rearrange("(p t) -> p t", t=T))
+        nc.scalar.dma_start(out=gb[:, 1, 0:T], in_=beta.rearrange("(p t) -> p t", t=T))
+        nc.scalar.dma_start(out=b2z[0:1, :], in_=b2.rearrange("(a o) -> a o", a=1))
+        for i in range(len(LOAD_BOUNDS) - 1):
+            g0, g1 = LOAD_BOUNDS[i], LOAD_BOUNDS[i + 1]
+            nc.sync.dma_start(out=Y[:, g0:g1, :], in_=yv[:, g0:g1, :])
+            if i == 1:
+                nc.sync.dma_start(out=w_sb[:], in_=W2.rearrange("(h o) k -> o h k", o=P))
+        nc.vector.memset(one1[:], 1.0)
+        nc.scalar.activation(out=warm[:], in_=one1[:], func=ACT.Sqrt)
+        nc.vector.memset(ones[:], 1.0)
+        nc.vector.memset(eps[:], BN_EPS)
+        nc.vector.memset(tiny[:], 1e-30)
+        make_identity(nc, ident[:])
+
+        def transposes(dst, g0, n, t):
+            for j in range(n):
+                nc.tensor.transpose(
+                    dst[:, j * P : (j + 1) * P], Y[:, g0 + j, t:K:T], ident[:]
+                )
+
+        with ExitStack() as ph1:
+            jpool = ph1.enter_context(tc.tile_pool(name="jpool", bufs=2))
+            pss = ph1.enter_context(tc.psum_pool(name="pss", bufs=1))
+            pst = ph1.enter_context(tc.psum_pool(name="pst", bufs=6))
+            sx_ps = pss.tile([P, (NU // SUMQ) * SP], F32, name="sx_ps")
+
+            m0_ps = pss.tile([P, SP], F32, tag="setup")
+            for t in range(SP):
+                nc.tensor.matmul(
+                    out=m0_ps[:, t : t + 1],
+                    lhsT=Y[:, 0, t:K:T],
+                    rhs=ones[:, 0:1],
+                    start=True,
+                    stop=True,
+                )
+            nc.scalar.activation(out=negm0[:], in_=m0_ps[:], func=ACT.Copy, scale=-1.0 / P)
+
+            for q in range(NU):
+                for t in range(T):
+                    tp = pst.tile([P, UC], BF16, tag="tp")
+                    transposes(tp, q * UNIT, UNIT, t)
+                    if t < SP:
+                        junk = jpool.tile([P, UC], BF16, tag="junk")
+                        nc.scalar.activation(
+                            out=junk[:],
+                            in_=tp[:],
+                            func=ACT.Square,
+                            bias=negm0[:, t : t + 1],
+                            accum_out=sq[:, t * NU + q : t * NU + q + 1],
+                        )
+                    else:
+                        nc.vector.bn_stats(out=st[:, t - SP, q, :], in_=tp[:])
+                if q % SUMQ == SUMQ - 1:
+                    blk = q // SUMQ
+                    ng = SUMQ * UNIT
+                    for t in range(SP):
+                        col = blk * SP + t
+                        for j in range(ng):
+                            nc.tensor.matmul(
+                                out=sx_ps[:, col : col + 1],
+                                lhsT=Y[:, blk * ng + j, t:K:T],
+                                rhs=ones[:, 0:1],
+                                start=(j == 0),
+                                stop=(j == ng - 1),
+                            )
+                if q == 2:
+                    wt_ps = pss.tile([P, T, O], BF16, tag="setup")
+                    for t in range(T):
+                        for h in range(2):
+                            nc.tensor.transpose(
+                                wt_ps[:, t, h * P : (h + 1) * P],
+                                w_sb[:, h, t:K:T],
+                                ident[:],
+                            )
+                    nc.scalar.copy(out=wt_sb[:], in_=wt_ps[:])
+                    nc.gpsimd.tensor_copy(out=wg[:], in_=wt_sb[:].rearrange("p t o -> p o t"))
+                if q == 6:
+                    nc.scalar.copy(out=gbT[:].rearrange("p (a t) -> p a t", t=T), in_=gb[:, :, 0:T])
+                    b2_ps = pss.tile([P, O], F32, tag="setup")
+                    nc.tensor.matmul(out=b2_ps[:], lhsT=ones[:], rhs=b2z[:], start=True, stop=True)
+                    for h in range(2):
+                        nc.scalar.copy(out=b2b[:, h, :], in_=b2_ps[:])
+
+            nc.vector.tensor_reduce(
+                out=sxs[:], in_=sx_ps[:].rearrange("p (k t) -> p t k", t=SP), axis=AX.X, op=ALU.add
+            )
+            nc.vector.bn_aggr(out=mv[:, SP, :], in_=st[:, 0].rearrange("p q s -> p (q s)"))
+            nc.vector.scalar_tensor_tensor(
+                out=dm[:], in0=sxs[:], scalar=1.0 / B, in1=negm0[:], op0=ALU.mult, op1=ALU.add
+            )
+            nc.vector.bn_aggr(out=mv[:, SP + 1, :], in_=st[:, 1].rearrange("p q s -> p (q s)"))
+            nc.vector.tensor_tensor(out=dm2[:], in0=dm[:], in1=dm[:], op=ALU.mult)
+            nc.vector.tensor_reduce(
+                out=sqs[:], in_=sq[:].rearrange("p (t q) -> p t q", q=NU), axis=AX.X, op=ALU.add
+            )
+            nc.vector.tensor_tensor(out=mv[:, 0:SP, 0], in0=dm[:], in1=negm0[:], op=ALU.subtract)
+            nc.vector.scalar_tensor_tensor(
+                out=mv[:, 0:SP, 1], in0=sqs[:], scalar=1.0 / B, in1=dm2[:], op0=ALU.mult, op1=ALU.subtract
+            )
+            nc.scalar.activation(out=std[:], in_=mv[:, :, 1], func=ACT.Sqrt, bias=eps[:, 0:1])
+            nc.vector.scalar_tensor_tensor(
+                out=nmg[:], in0=mv[:, :, 0], scalar=-1.0, in1=gbT[:, 0:T], op0=ALU.mult, op1=ALU.mult
+            )
+            nc.vector.quantize_mx(
+                out=w_codes[:].bitcast(FP8X4),
+                scales=w_scales[:],
+                in_=wg[:].rearrange("p o t -> p (o t)"),
+            )
+            nc.vector.reciprocal(out=rstd[:], in_=std[:])
+
+        zpool = ctx.enter_context(tc.tile_pool(name="zpool", bufs=2))
+        gpool = ctx.enter_context(tc.tile_pool(name="gpool", bufs=3))
+        qpool = ctx.enter_context(tc.tile_pool(name="qpool", bufs=3))
+        ppool = ctx.enter_context(tc.tile_pool(name="ppool", bufs=5))
+        spool = ctx.enter_context(tc.tile_pool(name="spool", bufs=5))
+        kpool = ctx.enter_context(tc.tile_pool(name="kpool", bufs=2))
+        ptq = ctx.enter_context(tc.psum_pool(name="ptq", bufs=T))
+        psm = ctx.enter_context(tc.psum_pool(name="psm", bufs=CMAX // 2))
+        NCH = len(CHUNKS)
+        starts = [sum(CHUNKS[:c]) for c in range(NCH)]
+        Xs, Zs, Gs, Cs, Ss, As, Ps, Ns, RIs = {}, {}, {}, {}, {}, {}, {}, {}, {}
+
+        def transpose_chunk(c):
+            Xs[c] = []
+            for t in range(T):
+                tq = ptq.tile([P, CMAX * P], BF16, tag="tq", name="tq")
+                transposes(tq, starts[c], CHUNKS[c], t)
+                Xs[c].append(tq)
+
+        def affine(c):
+            n = CHUNKS[c] * P
+            Zs[c] = zpool.tile([P, T, CMAX * P], BF16, tag="Z", name="Z")
+            for t in range(T):
+                nc.vector.tensor_scalar(
+                    out=Zs[c][:, t, 0:n],
+                    in0=Xs[c][t][:, 0:n],
+                    scalar1=sc[:, t : t + 1],
+                    scalar2=sh[:, t : t + 1],
+                    op0=ALU.mult,
+                    op1=ALU.add,
+                )
+
+        def regroup(c):
+            n = CHUNKS[c] * P
+            cv = 3 * n // 8
+            Gs[c] = gpool.tile([P, CMAX * P, T], BF16, tag="Gt", name="Gt", align_bytes=64)
+            nc.vector.tensor_scalar(
+                out=Gs[c][:, 0:cv, :].rearrange("p (c i) t -> p c t i", i=4),
+                in0=Zs[c][:, :, 0:cv].rearrange("p t (c i) -> p c t i", i=4),
+                scalar1=0.0,
+                scalar2=None,
+                op0=ALU.max,
+            )
+            nc.scalar.activation(
+                out=Gs[c][:, cv:n, :].rearrange("p (c i) t -> p c t i", i=4),
+                in_=Zs[c][:, :, cv:n].rearrange("p t (c i) -> p c t i", i=4),
+                func=ACT.Relu,
+            )
+
+        def quantise_multiply(c):
+            n = CHUNKS[c] * P
+            Cs[c] = qpool.tile([P, CMAX * P], U32, tag="codes", name="codes", align_bytes=64)
+            Ss[c] = qpool.tile([P, CMAX * P], U8, tag="scales", name="scales", align_bytes=64)
+            nc.vector.quantize_mx(
+                out=Cs[c][:, 0:n].bitcast(FP8X4),
+                scales=Ss[c][:, 0:n],
+                in_=Gs[c][:, 0:n, :].rearrange("p b t -> p (b t)"),
+            )
+            As[c] = []
+            for i in range(CHUNKS[c] // 2):
+                acc = psm.tile([P, 2, O], F32, tag="acc", name="acc")
+                As[c].append(acc)
+                for h in range(2):
+                    m = slice((2 * i + h) * P, (2 * i + h + 1) * P)
+                    nc.tensor.matmul_mx(
+                        out=acc[:, h, :],
+                        lhsT=Cs[c][:, m].bitcast(FP8X4),
+                        lhsT_scale=Ss[c][:, m],
+                        rhs=w_codes[:].bitcast(FP8X4),
+                        rhs_scale=w_scales[:],
+                        start=True,
+                        stop=True,
+                    )
+
+        def bias_squares(c):
+            ng = CHUNKS[c]
+            Ps[c] = ppool.tile([P, CMAX, O], F32, tag="Pt", name="Pt")
+            ss = spool.tile([P, CMAX], F32, tag="ss")
+            Ns[c] = spool.tile([P, CMAX], F32, tag="nrm", name="nrm")
+            for i in range(ng // 2):
+                nc.vector.tensor_tensor(
+                    out=Ps[c][:, 2 * i : 2 * i + 2, :], in0=As[c][i][:], in1=b2b[:], op=ALU.add
+                )
+            for r in range(ng):
+                junk2 = kpool.tile([P, O], BF16, tag="junk2")
+                nc.scalar.activation(
+                    out=junk2[:], in_=Ps[c][:, r, :], func=ACT.Square, accum_out=ss[:, r : r + 1]
+                )
+            nc.scalar.activation(out=Ns[c][:, 0:ng], in_=ss[:, 0:ng], func=ACT.Sqrt, bias=tiny[:, 0:1])
+
+        def clamp_norm(c):
+            ng = CHUNKS[c]
+            nrc = spool.tile([P, CMAX], F32, tag="nrc", name="nrc")
+            nc.vector.tensor_scalar(
+                out=nrc[:, 0:ng], in0=Ns[c][:, 0:ng], scalar1=L2_EPS, scalar2=None, op0=ALU.max
+            )
+            Ns[c] = nrc
+
+        def invert_norm(c):
+            ng = CHUNKS[c]
+            RIs[c] = spool.tile([P, CMAX], F32, tag="rinv", name="rinv")
+            nc.vector.reciprocal(out=RIs[c][:, 0:ng], in_=Ns[c][:, 0:ng])
+
+        def scale_store(c):
+            ng = CHUNKS[c]
+            last = c >= NCH - 2
+            for r in range(ng):
+                if r < ng // 2 and not last:
+                    nc.gpsimd.tensor_scalar(
+                        out=Ps[c][:, r, :],
+                        in0=Ps[c][:, r, :],
+                        scalar1=RIs[c][:, r : r + 1],
+                        scalar2=1.0,
+                        op0=ALU.mult,
+                        op1=ALU.mult,
+                    )
+                elif r < 3 * ng // 4 or last:
+                    nc.vector.tensor_scalar(
+                        out=Ps[c][:, r, :],
+                        in0=Ps[c][:, r, :],
+                        scalar1=RIs[c][:, r : r + 1],
+                        scalar2=None,
+                        op0=ALU.mult,
+                    )
+                else:
+                    nc.scalar.activation(
+                        out=Ps[c][:, r, :], in_=Ps[c][:, r, :], func=ACT.Copy, scale=RIs[c][:, r : r + 1]
+                    )
+            nc.sync.dma_start(out=ov[:, starts[c] : starts[c] + ng, :], in_=Ps[c][:, 0:ng, :])
+
+        transpose_chunk(0)
+        nc.vector.tensor_tensor(out=sc[:], in0=gbT[:, 0:T], in1=rstd[:], op=ALU.mult)
+        for t in range(T):
+            nc.vector.tensor_scalar(
+                out=sh[:, t : t + 1],
+                in0=rstd[:, t : t + 1],
+                scalar1=nmg[:, t : t + 1],
+                scalar2=gbT[:, T + t : T + t + 1],
+                op0=ALU.mult,
+                op1=ALU.add,
+            )
+        affine(0)
+        transpose_chunk(1)
+        for i in range(NCH + 2):
+            if i < NCH:
+                regroup(i)
+            if 0 <= i - 2:
+                clamp_norm(i - 2)
+            if i + 1 < NCH:
+                affine(i + 1)
+            if i + 2 < NCH:
+                transpose_chunk(i + 2)
+            if 0 <= i - 2:
+                invert_norm(i - 2)
+            if 0 <= i - 1 < NCH:
+                bias_squares(i - 1)
+            if 0 <= i - 2:
+                scale_store(i - 2)
+            if i < NCH:
+                quantise_multiply(i)

@@ -19,11 +19,12 @@ B = 8192
 K = 512
 O = 256
 T = K // P
+U = 2
 G = B // P
 UNIT = 4
 NU = G // UNIT
 UC = UNIT * P
-SP = 2
+E = 2
 SUMQ = 4
 BN_EPS = 1e-5
 L2_EPS = 1e-12
@@ -45,6 +46,7 @@ def tile_simclr_pa_t_kernel(tc, y_lin, gamma, beta, W2, b2, out):
         eps = const.tile([P, 1], F32, name="eps")
         tiny = const.tile([P, 1], F32, name="tiny")
         ident = const.tile([P, P], BF16, name="ident")
+        J = const.tile([P, 3 * P], F32, name="J")
         ones = const.tile([P, P], BF16, name="ones")
         gb = const.tile([P, 2, 16], BF16, name="gb")
         gbT = const.tile([P, 2 * T], F32, name="gbT")
@@ -55,14 +57,15 @@ def tile_simclr_pa_t_kernel(tc, y_lin, gamma, beta, W2, b2, out):
         wg = const.tile([P, O, T], BF16, name="wg", align_bytes=64)
         w_codes = const.tile([P, O], U32, name="w_codes", align_bytes=64)
         w_scales = const.tile([P, O], U8, name="w_scales", align_bytes=64)
-        negm0 = const.tile([P, SP], F32, name="negm0")
-        sq = const.tile([P, SP * NU], F32, name="sq")
-        st = const.tile([P, T - SP, NU, 6], F32, name="st")
-        mv = const.tile([P, T, 2], F32, name="mv")
-        sxs = const.tile([P, SP], F32, name="sxs")
-        sqs = const.tile([P, SP], F32, name="sqs")
-        dm = const.tile([P, SP], F32, name="dm")
-        dm2 = const.tile([P, SP], F32, name="dm2")
+        negm0 = const.tile([P, E], F32, name="negm0")
+        sq = const.tile([P, E * NU], F32, name="sq")
+        st = const.tile([P, 2 * NU, E, 3], F32, name="st")
+        agg = const.tile([P, E, 2], F32, name="agg")
+        mv = const.tile([P, U, 2, E], F32, name="mv")
+        sxs = const.tile([P, E], F32, name="sxs")
+        sqs = const.tile([P, E], F32, name="sqs")
+        dm = const.tile([P, E], F32, name="dm")
+        dm2 = const.tile([P, E], F32, name="dm2")
         nmg = const.tile([P, T], F32, name="nmg")
         std = const.tile([P, T], F32, name="std")
         rstd = const.tile([P, T], F32, name="rstd")
@@ -83,7 +86,11 @@ def tile_simclr_pa_t_kernel(tc, y_lin, gamma, beta, W2, b2, out):
         nc.vector.memset(ones[:], 1.0)
         nc.vector.memset(eps[:], BN_EPS)
         nc.vector.memset(tiny[:], 1e-30)
+        make_identity(nc, J[:, P : 2 * P])
         make_identity(nc, ident[:])
+        nc.vector.memset(J[:, 0:P], 0.0)
+        nc.vector.memset(J[:, 2 * P : 3 * P], 0.0)
+        Yw = Y[:].rearrange("p g k -> p (g k)").bitcast(F32)
 
         def transposes(dst, g0, n, t):
             for j in range(n):
@@ -95,13 +102,13 @@ def tile_simclr_pa_t_kernel(tc, y_lin, gamma, beta, W2, b2, out):
             jpool = ph1.enter_context(tc.tile_pool(name="jpool", bufs=2))
             pss = ph1.enter_context(tc.psum_pool(name="pss", bufs=1))
             pst = ph1.enter_context(tc.psum_pool(name="pst", bufs=6))
-            sx_ps = pss.tile([P, (NU // SUMQ) * SP], F32, name="sx_ps")
+            sx_ps = pss.tile([P, (NU // SUMQ) * E], F32, name="sx_ps")
 
-            m0_ps = pss.tile([P, SP], F32, tag="setup")
-            for t in range(SP):
+            m0_ps = pss.tile([P, E], F32, tag="setup")
+            for e in range(E):
                 nc.tensor.matmul(
-                    out=m0_ps[:, t : t + 1],
-                    lhsT=Y[:, 0, t:K:T],
+                    out=m0_ps[:, e : e + 1],
+                    lhsT=Y[:, 0, e : 2 * P : E],
                     rhs=ones[:, 0:1],
                     start=True,
                     stop=True,
@@ -109,29 +116,39 @@ def tile_simclr_pa_t_kernel(tc, y_lin, gamma, beta, W2, b2, out):
             nc.scalar.activation(out=negm0[:], in_=m0_ps[:], func=ACT.Copy, scale=-1.0 / P)
 
             for q in range(NU):
-                for t in range(T):
-                    tp = pst.tile([P, UC], BF16, tag="tp")
-                    transposes(tp, q * UNIT, UNIT, t)
-                    if t < SP:
-                        junk = jpool.tile([P, UC], BF16, tag="junk")
-                        nc.scalar.activation(
-                            out=junk[:],
-                            in_=tp[:],
-                            func=ACT.Square,
-                            bias=negm0[:, t : t + 1],
-                            accum_out=sq[:, t * NU + q : t * NU + q + 1],
+                for u in range(U):
+                    tp = pst.tile([P, UC], F32, tag="tp")
+                    for j in range(UNIT):
+                        w0 = (q * UNIT + j) * U * P + u * P
+                        nc.tensor.transpose(
+                            tp[:, j * P : (j + 1) * P], Yw[:, w0 : w0 + P], J[:, P : 2 * P]
                         )
+                    halves = tp[:].bitcast(BF16)
+                    if u == 0:
+                        for e in range(E):
+                            junk = jpool.tile([P, UC], BF16, tag="junk")
+                            nc.scalar.activation(
+                                out=junk[:],
+                                in_=halves[:, e : E * UC : E],
+                                func=ACT.Square,
+                                bias=negm0[:, e : e + 1],
+                                accum_out=sq[:, e * NU + q : e * NU + q + 1],
+                            )
                     else:
-                        nc.vector.bn_stats(out=st[:, t - SP, q, :], in_=tp[:])
+                        for h in range(2):
+                            nc.vector.bn_stats(
+                                out=st[:, 2 * q + h].rearrange("p e s -> p (e s)"),
+                                in_=halves[:, h * UC : (h + 1) * UC],
+                            )
                 if q % SUMQ == SUMQ - 1:
                     blk = q // SUMQ
                     ng = SUMQ * UNIT
-                    for t in range(SP):
-                        col = blk * SP + t
+                    for e in range(E):
+                        col = blk * E + e
                         for j in range(ng):
                             nc.tensor.matmul(
                                 out=sx_ps[:, col : col + 1],
-                                lhsT=Y[:, blk * ng + j, t:K:T],
+                                lhsT=Y[:, blk * ng + j, e : 2 * P : E],
                                 rhs=ones[:, 0:1],
                                 start=(j == 0),
                                 stop=(j == ng - 1),
@@ -155,24 +172,43 @@ def tile_simclr_pa_t_kernel(tc, y_lin, gamma, beta, W2, b2, out):
                         nc.scalar.copy(out=b2b[:, h, :], in_=b2_ps[:])
 
             nc.vector.tensor_reduce(
-                out=sxs[:], in_=sx_ps[:].rearrange("p (k t) -> p t k", t=SP), axis=AX.X, op=ALU.add
+                out=sxs[:], in_=sx_ps[:].rearrange("p (k e) -> p e k", e=E), axis=AX.X, op=ALU.add
             )
-            nc.vector.bn_aggr(out=mv[:, SP, :], in_=st[:, 0].rearrange("p q s -> p (q s)"))
+            nc.vector.bn_aggr(out=agg[:, 0, :], in_=st[:, :, 0, :])
             nc.vector.scalar_tensor_tensor(
                 out=dm[:], in0=sxs[:], scalar=1.0 / B, in1=negm0[:], op0=ALU.mult, op1=ALU.add
             )
-            nc.vector.bn_aggr(out=mv[:, SP + 1, :], in_=st[:, 1].rearrange("p q s -> p (q s)"))
+            nc.vector.bn_aggr(out=agg[:, 1, :], in_=st[:, :, 1, :])
             nc.vector.tensor_tensor(out=dm2[:], in0=dm[:], in1=dm[:], op=ALU.mult)
             nc.vector.tensor_reduce(
-                out=sqs[:], in_=sq[:].rearrange("p (t q) -> p t q", q=NU), axis=AX.X, op=ALU.add
+                out=sqs[:], in_=sq[:].rearrange("p (e q) -> p e q", q=NU), axis=AX.X, op=ALU.add
             )
-            nc.vector.tensor_tensor(out=mv[:, 0:SP, 0], in0=dm[:], in1=negm0[:], op=ALU.subtract)
+            nc.vector.tensor_tensor(out=mv[:, 0, 0, :], in0=dm[:], in1=negm0[:], op=ALU.subtract)
+            nc.vector.tensor_copy(out=mv[:, 1], in_=agg[:].rearrange("p e s -> p s e"))
             nc.vector.scalar_tensor_tensor(
-                out=mv[:, 0:SP, 1], in0=sqs[:], scalar=1.0 / B, in1=dm2[:], op0=ALU.mult, op1=ALU.subtract
+                out=mv[:, 0, 1, :], in0=sqs[:], scalar=1.0 / B, in1=dm2[:], op0=ALU.mult, op1=ALU.subtract
             )
-            nc.scalar.activation(out=std[:], in_=mv[:, :, 1], func=ACT.Sqrt, bias=eps[:, 0:1])
+            rel = pss.tile([P, U, 2, E], F32, tag="setup")
+            for v in range(U):
+                for u in range(U):
+                    c0 = P + v - P * u
+                    nc.tensor.matmul(
+                        out=rel[:, v].rearrange("p s e -> p (s e)"),
+                        lhsT=J[:, c0 : c0 + 2 * P - 1 : 2],
+                        rhs=mv[:, u].rearrange("p s e -> p (s e)"),
+                        start=(u == 0),
+                        stop=(u == U - 1),
+                    )
+            nc.scalar.activation(
+                out=std[:].rearrange("p (v e) -> p v e", e=E), in_=rel[:, :, 1, :], func=ACT.Sqrt, bias=eps[:, 0:1]
+            )
             nc.vector.scalar_tensor_tensor(
-                out=nmg[:], in0=mv[:, :, 0], scalar=-1.0, in1=gbT[:, 0:T], op0=ALU.mult, op1=ALU.mult
+                out=nmg[:].rearrange("p (v e) -> p v e", e=E),
+                in0=rel[:, :, 0, :],
+                scalar=-1.0,
+                in1=gbT[:, 0:T].rearrange("p (v e) -> p v e", e=E),
+                op0=ALU.mult,
+                op1=ALU.mult,
             )
             nc.vector.quantize_mx(
                 out=w_codes[:].bitcast(FP8X4),

@@ -67,6 +67,7 @@ def tile_simclr_pa_t_kernel(tc, y_lin, gamma, beta, W2, b2, out):
         dm = const.tile([P, E], F32, name="dm")
         dm2 = const.tile([P, E], F32, name="dm2")
         nmg = const.tile([P, T], F32, name="nmg")
+        nms = const.tile([P, T], F32, name="nms")
         std = const.tile([P, T], F32, name="std")
         rstd = const.tile([P, T], F32, name="rstd")
         sc = const.tile([P, T], F32, name="sc")
@@ -88,6 +89,7 @@ def tile_simclr_pa_t_kernel(tc, y_lin, gamma, beta, W2, b2, out):
         nc.vector.memset(tiny[:], 1e-30)
         make_identity(nc, J[:, P : 2 * P])
         make_identity(nc, ident[:])
+        nc.gpsimd.tensor_copy(out=gbT[:].rearrange("p (a t) -> p a t", t=T), in_=gb[:, :, 0:T])
         nc.vector.memset(J[:, 0:P], 0.0)
         nc.vector.memset(J[:, 2 * P : 3 * P], 0.0)
         Yw = Y[:].rearrange("p g k -> p (g k)").bitcast(F32)
@@ -98,11 +100,26 @@ def tile_simclr_pa_t_kernel(tc, y_lin, gamma, beta, W2, b2, out):
                     dst[:, j * P : (j + 1) * P], Y[:, g0 + j, t:K:T], ident[:]
                 )
 
+        ptq = ctx.enter_context(tc.psum_pool(name="ptq", bufs=T))
+
+        def transpose_chunk(c):
+            Xs[c] = []
+            for t in range(T):
+                tq = ptq.tile([P, CMAX * P], BF16, tag="tq", name="tq")
+                transposes(tq, starts[c], CHUNKS[c], t)
+                Xs[c].append(tq)
+
+        NCH = len(CHUNKS)
+        starts = [sum(CHUNKS[:c]) for c in range(NCH)]
+        Xs, Zs, Gs, Cs, Ss, As, Ps, Ns, RIs = {}, {}, {}, {}, {}, {}, {}, {}, {}
+
         with ExitStack() as ph1:
             jpool = ph1.enter_context(tc.tile_pool(name="jpool", bufs=2))
             pss = ph1.enter_context(tc.psum_pool(name="pss", bufs=1))
-            pst = ph1.enter_context(tc.psum_pool(name="pst", bufs=6))
-            sx_ps = pss.tile([P, (NU // SUMQ) * E], F32, name="sx_ps")
+            pst = ph1.enter_context(tc.psum_pool(name="pst", bufs=2))
+            small = pss.tile([P, 2 * O], F32, name="small")
+            sx_ps = small[:, 0 : (NU // SUMQ) * E]
+            b2_ps = small[:, O : 2 * O]
 
             m0_ps = pss.tile([P, E], F32, tag="setup")
             for e in range(E):
@@ -117,13 +134,18 @@ def tile_simclr_pa_t_kernel(tc, y_lin, gamma, beta, W2, b2, out):
 
             for q in range(NU):
                 for u in range(U):
-                    tp = pst.tile([P, UC], F32, tag="tp")
+                    if (q * U + u) % 3 < 2:
+                        wide = ptq.tile([P, CMAX * P], BF16, tag="tq", name="wide")
+                        tp = wide[:].bitcast(F32)
+                    else:
+                        narrow = pst.tile([P, UC], F32, tag="tp", name="narrow")
+                        tp = narrow[:]
                     for j in range(UNIT):
                         w0 = (q * UNIT + j) * U * P + u * P
                         nc.tensor.transpose(
                             tp[:, j * P : (j + 1) * P], Yw[:, w0 : w0 + P], J[:, P : 2 * P]
                         )
-                    halves = tp[:].bitcast(BF16)
+                    halves = tp.bitcast(BF16)
                     if u == 0:
                         for e in range(E):
                             junk = jpool.tile([P, UC], BF16, tag="junk")
@@ -147,7 +169,7 @@ def tile_simclr_pa_t_kernel(tc, y_lin, gamma, beta, W2, b2, out):
                         col = blk * E + e
                         for j in range(ng):
                             nc.tensor.matmul(
-                                out=sx_ps[:, col : col + 1],
+                                out=small[:, col : col + 1],
                                 lhsT=Y[:, blk * ng + j, e : 2 * P : E],
                                 rhs=ones[:, 0:1],
                                 start=(j == 0),
@@ -162,54 +184,54 @@ def tile_simclr_pa_t_kernel(tc, y_lin, gamma, beta, W2, b2, out):
                                 w_sb[:, h, t:K:T],
                                 ident[:],
                             )
-                    nc.scalar.copy(out=wt_sb[:], in_=wt_ps[:])
-                    nc.gpsimd.tensor_copy(out=wg[:], in_=wt_sb[:].rearrange("p t o -> p o t"))
-                if q == 6:
-                    nc.scalar.copy(out=gbT[:].rearrange("p (a t) -> p a t", t=T), in_=gb[:, :, 0:T])
-                    b2_ps = pss.tile([P, O], F32, tag="setup")
-                    nc.tensor.matmul(out=b2_ps[:], lhsT=ones[:], rhs=b2z[:], start=True, stop=True)
-                    for h in range(2):
-                        nc.scalar.copy(out=b2b[:, h, :], in_=b2_ps[:])
+                    nc.tensor.matmul(out=b2_ps, lhsT=ones[:], rhs=b2z[:], start=True, stop=True)
 
             nc.vector.tensor_reduce(
-                out=sxs[:], in_=sx_ps[:].rearrange("p (k e) -> p e k", e=E), axis=AX.X, op=ALU.add
+                out=sxs[:], in_=sx_ps.rearrange("p (k e) -> p e k", e=E), axis=AX.X, op=ALU.add
             )
+            for h in range(2):
+                nc.scalar.copy(out=b2b[:, h, :], in_=b2_ps)
+            nc.scalar.copy(out=wt_sb[:], in_=wt_ps[:])
+            nc.gpsimd.tensor_copy(out=wg[:], in_=wt_sb[:].rearrange("p t o -> p o t"))
             nc.vector.bn_aggr(out=agg[:, 0, :], in_=st[:, :, 0, :])
+            nc.vector.bn_aggr(out=agg[:, 1, :], in_=st[:, :, 1, :])
             nc.vector.scalar_tensor_tensor(
                 out=dm[:], in0=sxs[:], scalar=1.0 / B, in1=negm0[:], op0=ALU.mult, op1=ALU.add
             )
-            nc.vector.bn_aggr(out=agg[:, 1, :], in_=st[:, :, 1, :])
+            nc.vector.tensor_copy(out=mv[:, 1], in_=agg[:].rearrange("p e s -> p s e"))
             nc.vector.tensor_tensor(out=dm2[:], in0=dm[:], in1=dm[:], op=ALU.mult)
             nc.vector.tensor_reduce(
                 out=sqs[:], in_=sq[:].rearrange("p (e q) -> p e q", q=NU), axis=AX.X, op=ALU.add
             )
             nc.vector.tensor_tensor(out=mv[:, 0, 0, :], in0=dm[:], in1=negm0[:], op=ALU.subtract)
-            nc.vector.tensor_copy(out=mv[:, 1], in_=agg[:].rearrange("p e s -> p s e"))
             nc.vector.scalar_tensor_tensor(
                 out=mv[:, 0, 1, :], in0=sqs[:], scalar=1.0 / B, in1=dm2[:], op0=ALU.mult, op1=ALU.subtract
             )
-            rel = pss.tile([P, U, 2, E], F32, tag="setup")
+            transpose_chunk(0)
+            rels = []
             for v in range(U):
-                for u in range(U):
+                rel = pst.tile([P, UC], F32, tag="tp", name="rel")
+                rels.append(rel)
+            for u in (1, 0):
+                for v in range(U):
                     c0 = P + v - P * u
                     nc.tensor.matmul(
-                        out=rel[:, v].rearrange("p s e -> p (s e)"),
+                        out=rels[v][:, 0 : 2 * E],
                         lhsT=J[:, c0 : c0 + 2 * P - 1 : 2],
                         rhs=mv[:, u].rearrange("p s e -> p (s e)"),
-                        start=(u == 0),
-                        stop=(u == U - 1),
+                        start=(u == 1),
+                        stop=(u == 0),
                     )
-            nc.scalar.activation(
-                out=std[:].rearrange("p (v e) -> p v e", e=E), in_=rel[:, :, 1, :], func=ACT.Sqrt, bias=eps[:, 0:1]
-            )
-            nc.vector.scalar_tensor_tensor(
-                out=nmg[:].rearrange("p (v e) -> p v e", e=E),
-                in0=rel[:, :, 0, :],
-                scalar=-1.0,
-                in1=gbT[:, 0:T].rearrange("p (v e) -> p v e", e=E),
-                op0=ALU.mult,
-                op1=ALU.mult,
-            )
+            for v in range(U):
+                f = slice(v * E, (v + 1) * E)
+                nc.scalar.activation(
+                    out=std[:, f], in_=rels[v][:, E : 2 * E], func=ACT.Sqrt, bias=eps[:, 0:1]
+                )
+            for v in range(U):
+                f = slice(v * E, (v + 1) * E)
+                nc.vector.scalar_tensor_tensor(
+                    out=nmg[:, f], in0=rels[v][:, 0:E], scalar=-1.0, in1=gbT[:, f], op0=ALU.mult, op1=ALU.mult
+                )
             nc.vector.quantize_mx(
                 out=w_codes[:].bitcast(FP8X4),
                 scales=w_scales[:],
@@ -223,23 +245,20 @@ def tile_simclr_pa_t_kernel(tc, y_lin, gamma, beta, W2, b2, out):
         ppool = ctx.enter_context(tc.tile_pool(name="ppool", bufs=5))
         spool = ctx.enter_context(tc.tile_pool(name="spool", bufs=5))
         kpool = ctx.enter_context(tc.tile_pool(name="kpool", bufs=2))
-        ptq = ctx.enter_context(tc.psum_pool(name="ptq", bufs=T))
         psm = ctx.enter_context(tc.psum_pool(name="psm", bufs=CMAX // 2))
-        NCH = len(CHUNKS)
-        starts = [sum(CHUNKS[:c]) for c in range(NCH)]
-        Xs, Zs, Gs, Cs, Ss, As, Ps, Ns, RIs = {}, {}, {}, {}, {}, {}, {}, {}, {}
-
-        def transpose_chunk(c):
-            Xs[c] = []
-            for t in range(T):
-                tq = ptq.tile([P, CMAX * P], BF16, tag="tq", name="tq")
-                transposes(tq, starts[c], CHUNKS[c], t)
-                Xs[c].append(tq)
-
         def affine(c):
             n = CHUNKS[c] * P
             Zs[c] = zpool.tile([P, T, CMAX * P], BF16, tag="Z", name="Z")
             for t in range(T):
+                if c == 0 and t >= T // 2:
+                    nc.scalar.activation(
+                        out=Zs[c][:, t, 0:n],
+                        in_=Xs[c][t][:, 0:n],
+                        func=ACT.Identity,
+                        scale=sc[:, t : t + 1],
+                        bias=sh[:, t : t + 1],
+                    )
+                    continue
                 nc.vector.tensor_scalar(
                     out=Zs[c][:, t, 0:n],
                     in0=Xs[c][t][:, 0:n],
@@ -347,17 +366,9 @@ def tile_simclr_pa_t_kernel(tc, y_lin, gamma, beta, W2, b2, out):
                     )
             nc.sync.dma_start(out=ov[:, starts[c] : starts[c] + ng, :], in_=Ps[c][:, 0:ng, :])
 
-        transpose_chunk(0)
+        nc.vector.tensor_tensor(out=nms[:], in0=nmg[:], in1=rstd[:], op=ALU.mult)
         nc.vector.tensor_tensor(out=sc[:], in0=gbT[:, 0:T], in1=rstd[:], op=ALU.mult)
-        for t in range(T):
-            nc.vector.tensor_scalar(
-                out=sh[:, t : t + 1],
-                in0=rstd[:, t : t + 1],
-                scalar1=nmg[:, t : t + 1],
-                scalar2=gbT[:, T + t : T + t + 1],
-                op0=ALU.mult,
-                op1=ALU.add,
-            )
+        nc.vector.tensor_tensor(out=sh[:], in0=nms[:], in1=gbT[:, T : 2 * T], op=ALU.add)
         affine(0)
         transpose_chunk(1)
         for i in range(NCH + 2):

@@ -29,7 +29,7 @@ SUMQ = 4
 BN_EPS = 1e-5
 L2_EPS = 1e-12
 LOAD_BOUNDS = [0, 4, 8, 16, 24, 32, 40, 48, 56, 64]
-CHUNKS = [8, 8, 8, 8, 8, 8, 8, 4, 2, 2]
+CHUNKS = [4, 8, 8, 8, 8, 8, 8, 8, 2, 2]
 CMAX = 8
 
 
@@ -270,7 +270,7 @@ def tile_simclr_pa_t_kernel(tc, y_lin, gamma, beta, W2, b2, out):
 
         def regroup(c):
             n = CHUNKS[c] * P
-            cv = 3 * n // 8
+            cv = n // 4
             Gs[c] = gpool.tile([P, CMAX * P, T], BF16, tag="Gt", name="Gt", align_bytes=64)
             nc.vector.tensor_scalar(
                 out=Gs[c][:, 0:cv, :].rearrange("p (c i) t -> p c t i", i=4),
@@ -341,9 +341,11 @@ def tile_simclr_pa_t_kernel(tc, y_lin, gamma, beta, W2, b2, out):
 
         def scale_store(c):
             ng = CHUNKS[c]
+            ggp = ng // 2 if c == NCH - 3 else ng
+            gv = 3 * ng // 4 if c == NCH - 3 else ng
             last = c >= NCH - 2
             for r in range(ng):
-                if r < ng // 2 and not last:
+                if r < ggp and not last:
                     nc.gpsimd.tensor_scalar(
                         out=Ps[c][:, r, :],
                         in0=Ps[c][:, r, :],
@@ -352,7 +354,7 @@ def tile_simclr_pa_t_kernel(tc, y_lin, gamma, beta, W2, b2, out):
                         op0=ALU.mult,
                         op1=ALU.mult,
                     )
-                elif r < 3 * ng // 4 or last:
+                elif r < gv or last:
                     nc.vector.tensor_scalar(
                         out=Ps[c][:, r, :],
                         in0=Ps[c][:, r, :],
@@ -371,20 +373,19 @@ def tile_simclr_pa_t_kernel(tc, y_lin, gamma, beta, W2, b2, out):
         nc.vector.tensor_tensor(out=sh[:], in0=nms[:], in1=gbT[:, T : 2 * T], op=ALU.add)
         affine(0)
         transpose_chunk(1)
+        regroup(0)
         for i in range(NCH + 2):
-            if i < NCH:
-                regroup(i)
             if 0 <= i - 2:
                 clamp_norm(i - 2)
+                invert_norm(i - 2)
+                scale_store(i - 2)
             if i + 1 < NCH:
                 affine(i + 1)
             if i + 2 < NCH:
                 transpose_chunk(i + 2)
-            if 0 <= i - 2:
-                invert_norm(i - 2)
             if 0 <= i - 1 < NCH:
                 bias_squares(i - 1)
-            if 0 <= i - 2:
-                scale_store(i - 2)
             if i < NCH:
                 quantise_multiply(i)
+            if i + 1 < NCH:
+                regroup(i + 1)

@@ -28,8 +28,9 @@ E = 2
 SUMQ = 4
 BN_EPS = 1e-5
 L2_EPS = 1e-12
+F32_MAX = 3.4028234e38
 LOAD_BOUNDS = [0, 4, 8, 16, 24, 32, 40, 48, 56, 64]
-CHUNKS = [4, 8, 8, 8, 8, 8, 8, 8, 2, 2]
+CHUNKS = [4, 4, 8, 8, 8, 8, 8, 8, 4, 2, 2]
 CMAX = 8
 
 
@@ -44,7 +45,8 @@ def tile_simclr_pa_t_kernel(tc, y_lin, gamma, beta, W2, b2, out):
         one1 = const.tile([P, 1], F32, name="one1")
         warm = const.tile([P, 1], F32, name="warm")
         eps = const.tile([P, 1], F32, name="eps")
-        tiny = const.tile([P, 1], F32, name="tiny")
+        eps2 = const.tile([P, 1], F32, name="eps2")
+        neps2 = const.tile([P, 1], F32, name="neps2")
         ident = const.tile([P, P], BF16, name="ident")
         J = const.tile([P, 3 * P], F32, name="J")
         ones = const.tile([P, P], BF16, name="ones")
@@ -86,7 +88,8 @@ def tile_simclr_pa_t_kernel(tc, y_lin, gamma, beta, W2, b2, out):
         nc.scalar.activation(out=warm[:], in_=one1[:], func=ACT.Sqrt)
         nc.vector.memset(ones[:], 1.0)
         nc.vector.memset(eps[:], BN_EPS)
-        nc.vector.memset(tiny[:], 1e-30)
+        nc.vector.memset(eps2[:], L2_EPS * L2_EPS)
+        nc.vector.memset(neps2[:], -L2_EPS * L2_EPS)
         make_identity(nc, J[:, P : 2 * P])
         make_identity(nc, ident[:])
         nc.gpsimd.tensor_copy(out=gbT[:].rearrange("p (a t) -> p a t", t=T), in_=gb[:, :, 0:T])
@@ -102,12 +105,15 @@ def tile_simclr_pa_t_kernel(tc, y_lin, gamma, beta, W2, b2, out):
 
         ptq = ctx.enter_context(tc.psum_pool(name="ptq", bufs=T))
 
-        def transpose_chunk(c):
-            Xs[c] = []
+        def transpose_chunks(cs):
+            for c in cs:
+                Xs[c] = []
             for t in range(T):
                 tq = ptq.tile([P, CMAX * P], BF16, tag="tq", name="tq")
-                transposes(tq, starts[c], CHUNKS[c], t)
-                Xs[c].append(tq)
+                transposes(tq, starts[cs[0]], sum(CHUNKS[c] for c in cs), t)
+                for c in cs:
+                    r0 = (starts[c] - starts[cs[0]]) * P
+                    Xs[c].append(tq[:, r0 : r0 + CHUNKS[c] * P])
 
         NCH = len(CHUNKS)
         starts = [sum(CHUNKS[:c]) for c in range(NCH)]
@@ -207,7 +213,7 @@ def tile_simclr_pa_t_kernel(tc, y_lin, gamma, beta, W2, b2, out):
             nc.vector.scalar_tensor_tensor(
                 out=mv[:, 0, 1, :], in0=sqs[:], scalar=1.0 / B, in1=dm2[:], op0=ALU.mult, op1=ALU.subtract
             )
-            transpose_chunk(0)
+            transpose_chunks([0, 1])
             rels = []
             for v in range(U):
                 rel = pst.tile([P, UC], F32, tag="tp", name="rel")
@@ -227,6 +233,7 @@ def tile_simclr_pa_t_kernel(tc, y_lin, gamma, beta, W2, b2, out):
                 nc.scalar.activation(
                     out=std[:, f], in_=rels[v][:, E : 2 * E], func=ACT.Sqrt, bias=eps[:, 0:1]
                 )
+            nc.scalar.activation(out=warm[:], in_=one1[:], func=ACT.Abs_reciprocal_sqrt)
             for v in range(U):
                 f = slice(v * E, (v + 1) * E)
                 nc.vector.scalar_tensor_tensor(
@@ -270,15 +277,25 @@ def tile_simclr_pa_t_kernel(tc, y_lin, gamma, beta, W2, b2, out):
 
         def regroup(c):
             n = CHUNKS[c] * P
+            cg = n // 8 if 2 <= c < NCH - 3 else 0
             cv = n // 4
             Gs[c] = gpool.tile([P, CMAX * P, T], BF16, tag="Gt", name="Gt", align_bytes=64)
             nc.vector.tensor_scalar(
-                out=Gs[c][:, 0:cv, :].rearrange("p (c i) t -> p c t i", i=4),
-                in0=Zs[c][:, :, 0:cv].rearrange("p t (c i) -> p c t i", i=4),
+                out=Gs[c][:, cg:cv, :].rearrange("p (c i) t -> p c t i", i=4),
+                in0=Zs[c][:, :, cg:cv].rearrange("p t (c i) -> p c t i", i=4),
                 scalar1=0.0,
                 scalar2=None,
                 op0=ALU.max,
             )
+            if cg:
+                nc.gpsimd.tensor_scalar(
+                    out=Gs[c][:, 0:cg, :],
+                    in0=Zs[c][:, :, 0:cg].rearrange("p t b -> p b t"),
+                    scalar1=F32_MAX,
+                    scalar2=0.0,
+                    op0=ALU.min,
+                    op1=ALU.max,
+                )
             nc.scalar.activation(
                 out=Gs[c][:, cv:n, :].rearrange("p (c i) t -> p c t i", i=4),
                 in_=Zs[c][:, :, cv:n].rearrange("p t (c i) -> p c t i", i=4),
@@ -324,37 +341,23 @@ def tile_simclr_pa_t_kernel(tc, y_lin, gamma, beta, W2, b2, out):
                 nc.scalar.activation(
                     out=junk2[:], in_=Ps[c][:, r, :], func=ACT.Square, accum_out=ss[:, r : r + 1]
                 )
-            nc.scalar.activation(out=Ns[c][:, 0:ng], in_=ss[:, 0:ng], func=ACT.Sqrt, bias=tiny[:, 0:1])
-
-        def clamp_norm(c):
-            ng = CHUNKS[c]
-            nrc = spool.tile([P, CMAX], F32, tag="nrc", name="nrc")
-            nc.vector.tensor_scalar(
-                out=nrc[:, 0:ng], in0=Ns[c][:, 0:ng], scalar1=L2_EPS, scalar2=None, op0=ALU.max
-            )
-            Ns[c] = nrc
+            nc.scalar.activation(out=Ns[c][:, 0:ng], in_=ss[:, 0:ng], func=ACT.Relu, bias=neps2[:, 0:1])
 
         def invert_norm(c):
             ng = CHUNKS[c]
             RIs[c] = spool.tile([P, CMAX], F32, tag="rinv", name="rinv")
-            nc.vector.reciprocal(out=RIs[c][:, 0:ng], in_=Ns[c][:, 0:ng])
+            nc.scalar.activation(out=RIs[c][:, 0:ng], in_=Ns[c][:, 0:ng], func=ACT.Abs_reciprocal_sqrt, bias=eps2[:, 0:1])
 
         def scale_store(c):
             ng = CHUNKS[c]
-            ggp = ng // 2 if c == NCH - 3 else ng
-            gv = 3 * ng // 4 if c == NCH - 3 else ng
-            last = c >= NCH - 2
-            for r in range(ng):
-                if r < ggp and not last:
-                    nc.gpsimd.tensor_scalar(
-                        out=Ps[c][:, r, :],
-                        in0=Ps[c][:, r, :],
-                        scalar1=RIs[c][:, r : r + 1],
-                        scalar2=1.0,
-                        op0=ALU.mult,
-                        op1=ALU.mult,
-                    )
-                elif r < gv or last:
+            if c >= NCH - 2:
+                gp, vec = 0, ng // 2
+            elif c >= NCH - 4:
+                gp, vec = ng // 2, ng // 4
+            else:
+                gp, vec = 7 * ng // 8, ng - 7 * ng // 8
+            for r in range(gp, ng):
+                if r < gp + vec:
                     nc.vector.tensor_scalar(
                         out=Ps[c][:, r, :],
                         in0=Ps[c][:, r, :],
@@ -366,26 +369,39 @@ def tile_simclr_pa_t_kernel(tc, y_lin, gamma, beta, W2, b2, out):
                     nc.scalar.activation(
                         out=Ps[c][:, r, :], in_=Ps[c][:, r, :], func=ACT.Copy, scale=RIs[c][:, r : r + 1]
                     )
-            nc.sync.dma_start(out=ov[:, starts[c] : starts[c] + ng, :], in_=Ps[c][:, 0:ng, :])
+            for r in range(gp):
+                nc.gpsimd.tensor_scalar(
+                    out=Ps[c][:, r, :],
+                    in0=Ps[c][:, r, :],
+                    scalar1=RIs[c][:, r : r + 1],
+                    scalar2=1.0,
+                    op0=ALU.mult,
+                    op1=ALU.mult,
+                )
+            cuts = [0, ng] if c < NCH - 4 or gp == 0 else [gp, ng, 0, gp]
+            for k in range(0, len(cuts), 2):
+                r0, r1 = cuts[k], cuts[k + 1]
+                nc.sync.dma_start(
+                    out=ov[:, starts[c] + r0 : starts[c] + r1, :], in_=Ps[c][:, r0:r1, :]
+                )
 
         nc.vector.tensor_tensor(out=nms[:], in0=nmg[:], in1=rstd[:], op=ALU.mult)
         nc.vector.tensor_tensor(out=sc[:], in0=gbT[:, 0:T], in1=rstd[:], op=ALU.mult)
         nc.vector.tensor_tensor(out=sh[:], in0=nms[:], in1=gbT[:, T : 2 * T], op=ALU.add)
         affine(0)
-        transpose_chunk(1)
         regroup(0)
         for i in range(NCH + 2):
             if 0 <= i - 2:
-                clamp_norm(i - 2)
-                invert_norm(i - 2)
                 scale_store(i - 2)
             if i + 1 < NCH:
                 affine(i + 1)
             if i + 2 < NCH:
-                transpose_chunk(i + 2)
+                transpose_chunks([i + 2])
             if 0 <= i - 1 < NCH:
                 bias_squares(i - 1)
             if i < NCH:
                 quantise_multiply(i)
             if i + 1 < NCH:
                 regroup(i + 1)
+            if 0 <= i - 1 < NCH:
+                invert_norm(i - 1)

@@ -105,10 +105,10 @@ def tile_simclr_pa_t_kernel(tc, y_lin, gamma, beta, W2, b2, out):
 
         ptq = ctx.enter_context(tc.psum_pool(name="ptq", bufs=T))
 
-        def transpose_chunks(cs):
+        def transpose_chunks(cs, planes=range(T)):
             for c in cs:
-                Xs[c] = []
-            for t in range(T):
+                Xs.setdefault(c, [])
+            for t in planes:
                 tq = ptq.tile([P, CMAX * P], BF16, tag="tq", name="tq")
                 transposes(tq, starts[cs[0]], sum(CHUNKS[c] for c in cs), t)
                 for c in cs:
@@ -197,8 +197,6 @@ def tile_simclr_pa_t_kernel(tc, y_lin, gamma, beta, W2, b2, out):
             )
             for h in range(2):
                 nc.scalar.copy(out=b2b[:, h, :], in_=b2_ps)
-            nc.scalar.copy(out=wt_sb[:], in_=wt_ps[:])
-            nc.gpsimd.tensor_copy(out=wg[:], in_=wt_sb[:].rearrange("p t o -> p o t"))
             nc.vector.bn_aggr(out=agg[:, 0, :], in_=st[:, :, 0, :])
             nc.vector.bn_aggr(out=agg[:, 1, :], in_=st[:, :, 1, :])
             nc.vector.scalar_tensor_tensor(
@@ -213,7 +211,7 @@ def tile_simclr_pa_t_kernel(tc, y_lin, gamma, beta, W2, b2, out):
             nc.vector.scalar_tensor_tensor(
                 out=mv[:, 0, 1, :], in0=sqs[:], scalar=1.0 / B, in1=dm2[:], op0=ALU.mult, op1=ALU.subtract
             )
-            transpose_chunks([0, 1])
+            transpose_chunks([0, 1], range(T // 2))
             rels = []
             for v in range(U):
                 rel = pst.tile([P, UC], F32, tag="tp", name="rel")
@@ -228,22 +226,19 @@ def tile_simclr_pa_t_kernel(tc, y_lin, gamma, beta, W2, b2, out):
                         start=(u == 1),
                         stop=(u == 0),
                     )
+            transpose_chunks([0, 1], range(T // 2, T))
             for v in range(U):
                 f = slice(v * E, (v + 1) * E)
                 nc.scalar.activation(
                     out=std[:, f], in_=rels[v][:, E : 2 * E], func=ACT.Sqrt, bias=eps[:, 0:1]
                 )
-            nc.scalar.activation(out=warm[:], in_=one1[:], func=ACT.Abs_reciprocal_sqrt)
+            nc.scalar.copy(out=wt_sb[:], in_=wt_ps[:])
+            nc.gpsimd.tensor_copy(out=wg[:], in_=wt_sb[:].rearrange("p t o -> p o t"))
             for v in range(U):
                 f = slice(v * E, (v + 1) * E)
                 nc.vector.scalar_tensor_tensor(
                     out=nmg[:, f], in0=rels[v][:, 0:E], scalar=-1.0, in1=gbT[:, f], op0=ALU.mult, op1=ALU.mult
                 )
-            nc.vector.quantize_mx(
-                out=w_codes[:].bitcast(FP8X4),
-                scales=w_scales[:],
-                in_=wg[:].rearrange("p o t -> p (o t)"),
-            )
             nc.vector.reciprocal(out=rstd[:], in_=std[:])
 
         zpool = ctx.enter_context(tc.tile_pool(name="zpool", bufs=2))
@@ -257,7 +252,7 @@ def tile_simclr_pa_t_kernel(tc, y_lin, gamma, beta, W2, b2, out):
             n = CHUNKS[c] * P
             Zs[c] = zpool.tile([P, T, CMAX * P], BF16, tag="Z", name="Z")
             for t in range(T):
-                if c == 0 and t >= T // 2:
+                if c in (0, 2) and t >= T // 2:
                     nc.scalar.activation(
                         out=Zs[c][:, t, 0:n],
                         in_=Xs[c][t][:, 0:n],
@@ -278,7 +273,7 @@ def tile_simclr_pa_t_kernel(tc, y_lin, gamma, beta, W2, b2, out):
         def regroup(c):
             n = CHUNKS[c] * P
             cg = n // 8 if 2 <= c < NCH - 3 else 0
-            cv = n // 4
+            cv = 5 * n // 16
             Gs[c] = gpool.tile([P, CMAX * P, T], BF16, tag="Gt", name="Gt", align_bytes=64)
             nc.vector.tensor_scalar(
                 out=Gs[c][:, cg:cv, :].rearrange("p (c i) t -> p c t i", i=4),
@@ -355,7 +350,7 @@ def tile_simclr_pa_t_kernel(tc, y_lin, gamma, beta, W2, b2, out):
             elif c >= NCH - 4:
                 gp, vec = ng // 2, ng // 4
             else:
-                gp, vec = 7 * ng // 8, ng - 7 * ng // 8
+                gp, vec = ng, 0
             for r in range(gp, ng):
                 if r < gp + vec:
                     nc.vector.tensor_scalar(
@@ -389,16 +384,22 @@ def tile_simclr_pa_t_kernel(tc, y_lin, gamma, beta, W2, b2, out):
         nc.vector.tensor_tensor(out=sc[:], in0=gbT[:, 0:T], in1=rstd[:], op=ALU.mult)
         nc.vector.tensor_tensor(out=sh[:], in0=nms[:], in1=gbT[:, T : 2 * T], op=ALU.add)
         affine(0)
-        regroup(0)
         for i in range(NCH + 2):
-            if 0 <= i - 2:
-                scale_store(i - 2)
             if i + 1 < NCH:
                 affine(i + 1)
             if i + 2 < NCH:
                 transpose_chunks([i + 2])
             if 0 <= i - 1 < NCH:
                 bias_squares(i - 1)
+            if i == 0:
+                regroup(0)
+                nc.vector.quantize_mx(
+                    out=w_codes[:].bitcast(FP8X4),
+                    scales=w_scales[:],
+                    in_=wg[:].rearrange("p o t -> p (o t)"),
+                )
+            if 0 <= i - 2:
+                scale_store(i - 2)
             if i < NCH:
                 quantise_multiply(i)
             if i + 1 < NCH:

@@ -28,7 +28,6 @@ E = 2
 SUMQ = 4
 BN_EPS = 1e-5
 L2_EPS = 1e-12
-F32_MAX = 3.4028234e38
 LOAD_BOUNDS = [0, 4, 8, 16, 24, 32, 40, 48, 56, 64]
 CHUNKS = [4, 4, 8, 8, 8, 8, 8, 8, 4, 2, 2]
 CMAX = 8
@@ -45,8 +44,7 @@ def tile_simclr_pa_t_kernel(tc, y_lin, gamma, beta, W2, b2, out):
         one1 = const.tile([P, 1], F32, name="one1")
         warm = const.tile([P, 1], F32, name="warm")
         eps = const.tile([P, 1], F32, name="eps")
-        eps2 = const.tile([P, 1], F32, name="eps2")
-        neps2 = const.tile([P, 1], F32, name="neps2")
+        tiny = const.tile([P, 1], F32, name="tiny")
         ident = const.tile([P, P], BF16, name="ident")
         J = const.tile([P, 3 * P], F32, name="J")
         ones = const.tile([P, P], BF16, name="ones")
@@ -88,8 +86,7 @@ def tile_simclr_pa_t_kernel(tc, y_lin, gamma, beta, W2, b2, out):
         nc.scalar.activation(out=warm[:], in_=one1[:], func=ACT.Sqrt)
         nc.vector.memset(ones[:], 1.0)
         nc.vector.memset(eps[:], BN_EPS)
-        nc.vector.memset(eps2[:], L2_EPS * L2_EPS)
-        nc.vector.memset(neps2[:], -L2_EPS * L2_EPS)
+        nc.vector.memset(tiny[:], 1e-30)
         make_identity(nc, J[:, P : 2 * P])
         make_identity(nc, ident[:])
         nc.gpsimd.tensor_copy(out=gbT[:].rearrange("p (a t) -> p a t", t=T), in_=gb[:, :, 0:T])
@@ -211,6 +208,8 @@ def tile_simclr_pa_t_kernel(tc, y_lin, gamma, beta, W2, b2, out):
             nc.vector.scalar_tensor_tensor(
                 out=mv[:, 0, 1, :], in0=sqs[:], scalar=1.0 / B, in1=dm2[:], op0=ALU.mult, op1=ALU.subtract
             )
+            nc.vector.tensor_copy(out=wt_sb[:], in_=wt_ps[:])
+            nc.gpsimd.tensor_copy(out=wg[:], in_=wt_sb[:].rearrange("p t o -> p o t"))
             transpose_chunks([0, 1], range(T // 2))
             rels = []
             for v in range(U):
@@ -232,8 +231,7 @@ def tile_simclr_pa_t_kernel(tc, y_lin, gamma, beta, W2, b2, out):
                 nc.scalar.activation(
                     out=std[:, f], in_=rels[v][:, E : 2 * E], func=ACT.Sqrt, bias=eps[:, 0:1]
                 )
-            nc.scalar.copy(out=wt_sb[:], in_=wt_ps[:])
-            nc.gpsimd.tensor_copy(out=wg[:], in_=wt_sb[:].rearrange("p t o -> p o t"))
+            nc.scalar.activation(out=warm[:], in_=one1[:], func=ACT.Abs_reciprocal_sqrt)
             for v in range(U):
                 f = slice(v * E, (v + 1) * E)
                 nc.vector.scalar_tensor_tensor(
@@ -272,25 +270,15 @@ def tile_simclr_pa_t_kernel(tc, y_lin, gamma, beta, W2, b2, out):
 
         def regroup(c):
             n = CHUNKS[c] * P
-            cg = n // 8 if 2 <= c < NCH - 3 else 0
-            cv = 5 * n // 16
+            cv = n // 4
             Gs[c] = gpool.tile([P, CMAX * P, T], BF16, tag="Gt", name="Gt", align_bytes=64)
             nc.vector.tensor_scalar(
-                out=Gs[c][:, cg:cv, :].rearrange("p (c i) t -> p c t i", i=4),
-                in0=Zs[c][:, :, cg:cv].rearrange("p t (c i) -> p c t i", i=4),
+                out=Gs[c][:, 0:cv, :].rearrange("p (c i) t -> p c t i", i=4),
+                in0=Zs[c][:, :, 0:cv].rearrange("p t (c i) -> p c t i", i=4),
                 scalar1=0.0,
                 scalar2=None,
                 op0=ALU.max,
             )
-            if cg:
-                nc.gpsimd.tensor_scalar(
-                    out=Gs[c][:, 0:cg, :],
-                    in0=Zs[c][:, :, 0:cg].rearrange("p t b -> p b t"),
-                    scalar1=F32_MAX,
-                    scalar2=0.0,
-                    op0=ALU.min,
-                    op1=ALU.max,
-                )
             nc.scalar.activation(
                 out=Gs[c][:, cv:n, :].rearrange("p (c i) t -> p c t i", i=4),
                 in_=Zs[c][:, :, cv:n].rearrange("p t (c i) -> p c t i", i=4),
@@ -326,7 +314,6 @@ def tile_simclr_pa_t_kernel(tc, y_lin, gamma, beta, W2, b2, out):
             ng = CHUNKS[c]
             Ps[c] = ppool.tile([P, CMAX, O], F32, tag="Pt", name="Pt")
             ss = spool.tile([P, CMAX], F32, tag="ss")
-            Ns[c] = spool.tile([P, CMAX], F32, tag="nrm", name="nrm")
             for i in range(ng // 2):
                 nc.vector.tensor_tensor(
                     out=Ps[c][:, 2 * i : 2 * i + 2, :], in0=As[c][i][:], in1=b2b[:], op=ALU.add
@@ -336,21 +323,45 @@ def tile_simclr_pa_t_kernel(tc, y_lin, gamma, beta, W2, b2, out):
                 nc.scalar.activation(
                     out=junk2[:], in_=Ps[c][:, r, :], func=ACT.Square, accum_out=ss[:, r : r + 1]
                 )
-            nc.scalar.activation(out=Ns[c][:, 0:ng], in_=ss[:, 0:ng], func=ACT.Relu, bias=neps2[:, 0:1])
+            Ns[c] = ss
 
         def invert_norm(c):
             ng = CHUNKS[c]
             RIs[c] = spool.tile([P, CMAX], F32, tag="rinv", name="rinv")
-            nc.scalar.activation(out=RIs[c][:, 0:ng], in_=Ns[c][:, 0:ng], func=ACT.Abs_reciprocal_sqrt, bias=eps2[:, 0:1])
+            nc.scalar.activation(
+                out=RIs[c][:, 0:ng], in_=Ns[c][:, 0:ng], func=ACT.Abs_reciprocal_sqrt, bias=tiny[:, 0:1]
+            )
+
+        def clamp_norm(c):
+            ng = CHUNKS[c]
+            rc = spool.tile([P, CMAX], F32, tag="rclamp", name="rc")
+            nc.vector.tensor_scalar(
+                out=rc[:, 0:ng], in0=RIs[c][:, 0:ng], scalar1=1.0 / L2_EPS, scalar2=None, op0=ALU.min
+            )
+            RIs[c] = rc
+
+        def shares(c):
+            ng = CHUNKS[c]
+            if c >= NCH - 2:
+                return 0, ng // 2
+            if c >= NCH - 4:
+                return ng // 2, ng // 4
+            return 7 * ng // 8, ng - 7 * ng // 8
+
+        def scale_gpsimd(c):
+            for r in range(shares(c)[0]):
+                nc.gpsimd.tensor_scalar(
+                    out=Ps[c][:, r, :],
+                    in0=Ps[c][:, r, :],
+                    scalar1=RIs[c][:, r : r + 1],
+                    scalar2=1.0,
+                    op0=ALU.mult,
+                    op1=ALU.mult,
+                )
 
         def scale_store(c):
             ng = CHUNKS[c]
-            if c >= NCH - 2:
-                gp, vec = 0, ng // 2
-            elif c >= NCH - 4:
-                gp, vec = ng // 2, ng // 4
-            else:
-                gp, vec = ng, 0
+            gp, vec = shares(c)
             for r in range(gp, ng):
                 if r < gp + vec:
                     nc.vector.tensor_scalar(
@@ -364,15 +375,6 @@ def tile_simclr_pa_t_kernel(tc, y_lin, gamma, beta, W2, b2, out):
                     nc.scalar.activation(
                         out=Ps[c][:, r, :], in_=Ps[c][:, r, :], func=ACT.Copy, scale=RIs[c][:, r : r + 1]
                     )
-            for r in range(gp):
-                nc.gpsimd.tensor_scalar(
-                    out=Ps[c][:, r, :],
-                    in0=Ps[c][:, r, :],
-                    scalar1=RIs[c][:, r : r + 1],
-                    scalar2=1.0,
-                    op0=ALU.mult,
-                    op1=ALU.mult,
-                )
             cuts = [0, ng] if c < NCH - 4 or gp == 0 else [gp, ng, 0, gp]
             for k in range(0, len(cuts), 2):
                 r0, r1 = cuts[k], cuts[k + 1]
@@ -385,6 +387,9 @@ def tile_simclr_pa_t_kernel(tc, y_lin, gamma, beta, W2, b2, out):
         nc.vector.tensor_tensor(out=sh[:], in0=nms[:], in1=gbT[:, T : 2 * T], op=ALU.add)
         affine(0)
         for i in range(NCH + 2):
+            if 0 <= i - 2:
+                clamp_norm(i - 2)
+                scale_gpsimd(i - 2)
             if i + 1 < NCH:
                 affine(i + 1)
             if i + 2 < NCH:
@@ -400,9 +405,9 @@ def tile_simclr_pa_t_kernel(tc, y_lin, gamma, beta, W2, b2, out):
                 )
             if 0 <= i - 2:
                 scale_store(i - 2)
+            if 0 <= i - 1 < NCH:
+                invert_norm(i - 1)
             if i < NCH:
                 quantise_multiply(i)
             if i + 1 < NCH:
                 regroup(i + 1)
-            if 0 <= i - 1 < NCH:
-                invert_norm(i - 1)

@@ -22,13 +22,14 @@ T = K // P
 U = 2
 G = B // P
 UNIT = 4
-NU = G // UNIT
 UC = UNIT * P
 E = 2
-SUMQ = 4
+SUMG = 4
 BN_EPS = 1e-5
 L2_EPS = 1e-12
-LOAD_BOUNDS = [0, 4, 8, 16, 24, 32, 40, 48, 56, 64]
+UNITS = [2, 2] + [UNIT] * 15
+NU = len(UNITS)
+LOAD_BOUNDS = [0, 2, 4, 8, 16, 24, 32, 40, 48, 56, 64]
 CHUNKS = [4, 4, 8, 8, 8, 8, 8, 8, 4, 2, 2]
 CMAX = 8
 
@@ -59,7 +60,7 @@ def tile_simclr_pa_t_kernel(tc, y_lin, gamma, beta, W2, b2, out):
         w_scales = const.tile([P, O], U8, name="w_scales", align_bytes=64)
         negm0 = const.tile([P, E], F32, name="negm0")
         sq = const.tile([P, E * NU], F32, name="sq")
-        st = const.tile([P, 2 * NU, E, 3], F32, name="st")
+        st = const.tile([P, G // 2, E, 3], F32, name="st")
         agg = const.tile([P, E, 2], F32, name="agg")
         mv = const.tile([P, U, 2, E], F32, name="mv")
         sxs = const.tile([P, E], F32, name="sxs")
@@ -80,7 +81,7 @@ def tile_simclr_pa_t_kernel(tc, y_lin, gamma, beta, W2, b2, out):
         for i in range(len(LOAD_BOUNDS) - 1):
             g0, g1 = LOAD_BOUNDS[i], LOAD_BOUNDS[i + 1]
             nc.sync.dma_start(out=Y[:, g0:g1, :], in_=yv[:, g0:g1, :])
-            if i == 1:
+            if i == 2:
                 nc.sync.dma_start(out=w_sb[:], in_=W2.rearrange("(h o) k -> o h k", o=P))
         nc.vector.memset(one1[:], 1.0)
         nc.scalar.activation(out=warm[:], in_=one1[:], func=ACT.Sqrt)
@@ -121,7 +122,7 @@ def tile_simclr_pa_t_kernel(tc, y_lin, gamma, beta, W2, b2, out):
             pss = ph1.enter_context(tc.psum_pool(name="pss", bufs=1))
             pst = ph1.enter_context(tc.psum_pool(name="pst", bufs=2))
             small = pss.tile([P, 2 * O], F32, name="small")
-            sx_ps = small[:, 0 : (NU // SUMQ) * E]
+            sx_ps = small[:, 0 : (G // SUMG) * E]
             b2_ps = small[:, O : 2 * O]
 
             m0_ps = pss.tile([P, E], F32, tag="setup")
@@ -136,15 +137,17 @@ def tile_simclr_pa_t_kernel(tc, y_lin, gamma, beta, W2, b2, out):
             nc.scalar.activation(out=negm0[:], in_=m0_ps[:], func=ACT.Copy, scale=-1.0 / P)
 
             for q in range(NU):
-                for u in range(U):
-                    if (q * U + u) % 3 < 2:
+                g0, ng = sum(UNITS[:q]), UNITS[q]
+                n = ng * P
+                for u in (1, 0):
+                    if (q * U + 1 - u) % 3 < 2:
                         wide = ptq.tile([P, CMAX * P], BF16, tag="tq", name="wide")
                         tp = wide[:].bitcast(F32)
                     else:
                         narrow = pst.tile([P, UC], F32, tag="tp", name="narrow")
                         tp = narrow[:]
-                    for j in range(UNIT):
-                        w0 = (q * UNIT + j) * U * P + u * P
+                    for j in range(ng):
+                        w0 = (g0 + j) * U * P + u * P
                         nc.tensor.transpose(
                             tp[:, j * P : (j + 1) * P], Yw[:, w0 : w0 + P], J[:, P : 2 * P]
                         )
@@ -153,32 +156,31 @@ def tile_simclr_pa_t_kernel(tc, y_lin, gamma, beta, W2, b2, out):
                         for e in range(E):
                             junk = jpool.tile([P, UC], BF16, tag="junk")
                             nc.scalar.activation(
-                                out=junk[:],
-                                in_=halves[:, e : E * UC : E],
+                                out=junk[:, 0:n],
+                                in_=halves[:, e : E * n : E],
                                 func=ACT.Square,
                                 bias=negm0[:, e : e + 1],
                                 accum_out=sq[:, e * NU + q : e * NU + q + 1],
                             )
                     else:
-                        for h in range(2):
+                        for h in range(ng // 2):
                             nc.vector.bn_stats(
-                                out=st[:, 2 * q + h].rearrange("p e s -> p (e s)"),
+                                out=st[:, g0 // 2 + h].rearrange("p e s -> p (e s)"),
                                 in_=halves[:, h * UC : (h + 1) * UC],
                             )
-                if q % SUMQ == SUMQ - 1:
-                    blk = q // SUMQ
-                    ng = SUMQ * UNIT
+                if (g0 + ng) % SUMG == 0:
+                    blk = g0 // SUMG
                     for e in range(E):
                         col = blk * E + e
-                        for j in range(ng):
+                        for j in range(SUMG):
                             nc.tensor.matmul(
                                 out=small[:, col : col + 1],
-                                lhsT=Y[:, blk * ng + j, e : 2 * P : E],
+                                lhsT=Y[:, blk * SUMG + j, e : 2 * P : E],
                                 rhs=ones[:, 0:1],
                                 start=(j == 0),
-                                stop=(j == ng - 1),
+                                stop=(j == SUMG - 1),
                             )
-                if q == 2:
+                if q == 3:
                     wt_ps = pss.tile([P, T, O], BF16, tag="setup")
                     for t in range(T):
                         for h in range(2):
@@ -210,7 +212,7 @@ def tile_simclr_pa_t_kernel(tc, y_lin, gamma, beta, W2, b2, out):
             )
             nc.vector.tensor_copy(out=wt_sb[:], in_=wt_ps[:])
             nc.gpsimd.tensor_copy(out=wg[:], in_=wt_sb[:].rearrange("p t o -> p o t"))
-            transpose_chunks([0, 1], range(T // 2))
+            transpose_chunks([0, 1], range(T - 1))
             rels = []
             for v in range(U):
                 rel = pst.tile([P, UC], F32, tag="tp", name="rel")
@@ -225,7 +227,7 @@ def tile_simclr_pa_t_kernel(tc, y_lin, gamma, beta, W2, b2, out):
                         start=(u == 1),
                         stop=(u == 0),
                     )
-            transpose_chunks([0, 1], range(T // 2, T))
+            transpose_chunks([0, 1], range(T - 1, T))
             for v in range(U):
                 f = slice(v * E, (v + 1) * E)
                 nc.scalar.activation(
@@ -270,7 +272,7 @@ def tile_simclr_pa_t_kernel(tc, y_lin, gamma, beta, W2, b2, out):
 
         def regroup(c):
             n = CHUNKS[c] * P
-            cv = n // 4
+            cv = n // 2 if c < 2 or c >= NCH - 3 else n // 4
             Gs[c] = gpool.tile([P, CMAX * P, T], BF16, tag="Gt", name="Gt", align_bytes=64)
             nc.vector.tensor_scalar(
                 out=Gs[c][:, 0:cv, :].rearrange("p (c i) t -> p c t i", i=4),
@@ -319,6 +321,18 @@ def tile_simclr_pa_t_kernel(tc, y_lin, gamma, beta, W2, b2, out):
                     out=Ps[c][:, 2 * i : 2 * i + 2, :], in0=As[c][i][:], in1=b2b[:], op=ALU.add
                 )
             for r in range(ng):
+                if c == NCH - 1 and r % 2:
+                    junk3 = kpool.tile([P, O], F32, tag="junk3")
+                    nc.vector.scalar_tensor_tensor(
+                        out=junk3[:],
+                        in0=Ps[c][:, r, :],
+                        scalar=1.0,
+                        in1=Ps[c][:, r, :],
+                        op0=ALU.mult,
+                        op1=ALU.mult,
+                        accum_out=ss[:, r : r + 1],
+                    )
+                    continue
                 junk2 = kpool.tile([P, O], BF16, tag="junk2")
                 nc.scalar.activation(
                     out=junk2[:], in_=Ps[c][:, r, :], func=ACT.Square, accum_out=ss[:, r : r + 1]
@@ -346,7 +360,7 @@ def tile_simclr_pa_t_kernel(tc, y_lin, gamma, beta, W2, b2, out):
                 return 0, ng // 2
             if c >= NCH - 4:
                 return ng // 2, ng // 4
-            return 7 * ng // 8, ng - 7 * ng // 8
+            return ng, 0
 
         def scale_gpsimd(c):
             for r in range(shares(c)[0]):

@@ -24,12 +24,12 @@ G = B // P
 UNIT = 4
 UC = UNIT * P
 E = 2
-SUMG = 4
+SUMG = 16
 BN_EPS = 1e-5
 L2_EPS = 1e-12
 UNITS = [2, 2] + [UNIT] * 15
 NU = len(UNITS)
-LOAD_BOUNDS = [0, 2, 4, 8, 16, 24, 32, 40, 48, 56, 64]
+LOAD_BOUNDS = [0, 2, 4, 8, 12, 16, 24, 32, 40, 48, 56, 64]
 CHUNKS = [4, 4, 8, 8, 8, 8, 8, 8, 4, 2, 2]
 CMAX = 8
 
@@ -360,7 +360,7 @@ def tile_simclr_pa_t_kernel(tc, y_lin, gamma, beta, W2, b2, out):
                 return 0, ng // 2
             if c >= NCH - 4:
                 return ng // 2, ng // 4
-            return ng, 0
+            return 7 * ng // 8, ng - 7 * ng // 8
 
         def scale_gpsimd(c):
             for r in range(shares(c)[0]):
@@ -417,9 +417,11 @@ def tile_simclr_pa_t_kernel(tc, y_lin, gamma, beta, W2, b2, out):
                     scales=w_scales[:],
                     in_=wg[:].rearrange("p o t -> p (o t)"),
                 )
+            if NCH - 3 <= i - 1 < NCH:
+                invert_norm(i - 1)
             if 0 <= i - 2:
                 scale_store(i - 2)
-            if 0 <= i - 1 < NCH:
+            if 0 <= i - 1 < NCH - 3:
                 invert_norm(i - 1)
             if i < NCH:
                 quantise_multiply(i)

from contextlib import ExitStack

import concourse.mybir as mybir
from concourse.masks import make_identity

FLOPS = 2 * 8192 * 512 * 256

FP8X4 = mybir.dt.float8_e4m3fn_x4
BF16 = mybir.dt.bfloat16
F32 = mybir.dt.float32
U32 = mybir.dt.uint32
U8 = mybir.dt.uint8
ALU = mybir.AluOpType
ACT = mybir.ActivationFunctionType
AX = mybir.AxisListType

P = 128
B = 8192
K = 512
O = 256
T = K // P
U = 2
G = B // P
UNIT = 4
UC = UNIT * P
E = 2
SUMG = 16
BN_EPS = 1e-5
L2_EPS = 1e-12
UNITS = [2, 2] + [UNIT] * 15
NU = len(UNITS)
LOAD_BOUNDS = [0, 2, 4, 8, 12, 16, 24, 32, 40, 48, 56, 64]
CHUNKS = [4, 4, 8, 8, 8, 8, 8, 8, 4, 2, 2]
CMAX = 8


def tile_simclr_pa_t_kernel(tc, y_lin, gamma, beta, W2, b2, out):
    nc = tc.nc
    yv = y_lin.rearrange("(p g) k -> p g k", g=G)
    ov = out.rearrange("(p g) o -> p g o", g=G)
    with ExitStack() as ctx:
        ctx.enter_context(tc.manual_schedule())
        const = ctx.enter_context(tc.tile_pool(name="const", bufs=1))
        Y = const.tile([P, G, K], BF16, name="Y")
        one1 = const.tile([P, 1], F32, name="one1")
        warm = const.tile([P, 1], F32, name="warm")
        eps = const.tile([P, 1], F32, name="eps")
        tiny = const.tile([P, 1], F32, name="tiny")
        ident = const.tile([P, P], BF16, name="ident")
        J = const.tile([P, 3 * P], F32, name="J")
        ones = const.tile([P, P], BF16, name="ones")
        gb = const.tile([P, 2, 16], BF16, name="gb")
        gbT = const.tile([P, 2 * T], F32, name="gbT")
        b2z = const.tile([P, O], BF16, name="b2z")
        b2b = const.tile([P, 2, O], F32, name="b2b")
        w_sb = const.tile([P, 2, K], BF16, name="w_sb")
        wt_sb = const.tile([P, T, O], BF16, name="wt_sb")
        wg = const.tile([P, O, T], BF16, name="wg", align_bytes=64)
        w_codes = const.tile([P, O], U32, name="w_codes", align_bytes=64)
        w_scales = const.tile([P, O], U8, name="w_scales", align_bytes=64)
        negm0 = const.tile([P, E], F32, name="negm0")
        sq = const.tile([P, E * NU], F32, name="sq")
        st = const.tile([P, G // 2, E, 3], F32, name="st")
        agg = const.tile([P, E, 2], F32, name="agg")
        mv = const.tile([P, U, 2, E], F32, name="mv")
        sxs = const.tile([P, E], F32, name="sxs")
        sqs = const.tile([P, E], F32, name="sqs")
        dm = const.tile([P, E], F32, name="dm")
        dm2 = const.tile([P, E], F32, name="dm2")
        nmg = const.tile([P, T], F32, name="nmg")
        nms = const.tile([P, T], F32, name="nms")
        std = const.tile([P, T], F32, name="std")
        rstd = const.tile([P, T], F32, name="rstd")
        sc = const.tile([P, T], F32, name="sc")
        sh = const.tile([P, T], F32, name="sh")

        nc.vector.memset(b2z[:], 0.0)
        nc.scalar.dma_start(out=gb[:, 0, 0:T], in_=gamma.rearrange("(p t) -> p t", t=T))
        nc.scalar.dma_start(out=gb[:, 1, 0:T], in_=beta.rearrange("(p t) -> p t", t=T))
        nc.scalar.dma_start(out=b2z[0:1, :], in_=b2.rearrange("(a o) -> a o", a=1))
        for i in range(len(LOAD_BOUNDS) - 1):
            g0, g1 = LOAD_BOUNDS[i], LOAD_BOUNDS[i + 1]
            nc.sync.dma_start(out=Y[:, g0:g1, :], in_=yv[:, g0:g1, :])
            if i == 2:
                nc.sync.dma_start(out=w_sb[:], in_=W2.rearrange("(h o) k -> o h k", o=P))
        nc.vector.memset(one1[:], 1.0)
        nc.scalar.activation(out=warm[:], in_=one1[:], func=ACT.Sqrt)
        nc.vector.memset(ones[:], 1.0)
        nc.vector.memset(eps[:], BN_EPS)
        nc.vector.memset(tiny[:], 1e-30)
        make_identity(nc, J[:, P : 2 * P])
        make_identity(nc, ident[:])
        nc.gpsimd.tensor_copy(out=gbT[:].rearrange("p (a t) -> p a t", t=T), in_=gb[:, :, 0:T])
        nc.vector.memset(J[:, 0:P], 0.0)
        nc.vector.memset(J[:, 2 * P : 3 * P], 0.0)
        Yw = Y[:].rearrange("p g k -> p (g k)").bitcast(F32)

        def transposes(dst, g0, n, t):
            for j in range(n):
                nc.tensor.transpose(
                    dst[:, j * P : (j + 1) * P], Y[:, g0 + j, t:K:T], ident[:]
                )

        ptq = ctx.enter_context(tc.psum_pool(name="ptq", bufs=T))

        def transpose_chunks(cs, planes=range(T)):
            for c in cs:
                Xs.setdefault(c, [])
            for t in planes:
                tq = ptq.tile([P, CMAX * P], BF16, tag="tq", name="tq")
                transposes(tq, starts[cs[0]], sum(CHUNKS[c] for c in cs), t)
                for c in cs:
                    r0 = (starts[c] - starts[cs[0]]) * P
                    Xs[c].append(tq[:, r0 : r0 + CHUNKS[c] * P])

        NCH = len(CHUNKS)
        starts = [sum(CHUNKS[:c]) for c in range(NCH)]
        Xs, Zs, Gs, Cs, Ss, As, Ps, Ns, RIs = {}, {}, {}, {}, {}, {}, {}, {}, {}

        with ExitStack() as ph1:
            jpool = ph1.enter_context(tc.tile_pool(name="jpool", bufs=2))
            pss = ph1.enter_context(tc.psum_pool(name="pss", bufs=1))
            pst = ph1.enter_context(tc.psum_pool(name="pst", bufs=2))
            small = pss.tile([P, 2 * O], F32, name="small")
            sx_ps = small[:, 0 : (G // SUMG) * E]
            b2_ps = small[:, O : 2 * O]

            m0_ps = pss.tile([P, E], F32, tag="setup")
            for e in range(E):
                nc.tensor.matmul(
                    out=m0_ps[:, e : e + 1],
                    lhsT=Y[:, 0, e : 2 * P : E],
                    rhs=ones[:, 0:1],
                    start=True,
                    stop=True,
                )
            nc.scalar.activation(out=negm0[:], in_=m0_ps[:], func=ACT.Copy, scale=-1.0 / P)

            for q in range(NU):
                g0, ng = sum(UNITS[:q]), UNITS[q]
                n = ng * P
                for u in (1, 0):
                    if (q * U + 1 - u) % 3 < 2:
                        wide = ptq.tile([P, CMAX * P], BF16, tag="tq", name="wide")
                        tp = wide[:].bitcast(F32)
                    else:
                        narrow = pst.tile([P, UC], F32, tag="tp", name="narrow")
                        tp = narrow[:]
                    for j in range(ng):
                        w0 = (g0 + j) * U * P + u * P
                        nc.tensor.transpose(
                            tp[:, j * P : (j + 1) * P], Yw[:, w0 : w0 + P], J[:, P : 2 * P]
                        )
                    halves = tp.bitcast(BF16)
                    if u == 0:
                        for e in range(E):
                            junk = jpool.tile([P, UC], BF16, tag="junk")
                            nc.scalar.activation(
                                out=junk[:, 0:n],
                                in_=halves[:, e : E * n : E],
                                func=ACT.Square,
                                bias=negm0[:, e : e + 1],
                                accum_out=sq[:, e * NU + q : e * NU + q + 1],
                            )
                    else:
                        for h in range(ng // 2):
                            nc.vector.bn_stats(
                                out=st[:, g0 // 2 + h].rearrange("p e s -> p (e s)"),
                                in_=halves[:, h * UC : (h + 1) * UC],
                            )
                if (g0 + ng) % SUMG == 0:
                    blk = g0 // SUMG
                    for e in range(E):
                        col = blk * E + e
                        for j in range(SUMG):
                            nc.tensor.matmul(
                                out=small[:, col : col + 1],
                                lhsT=Y[:, blk * SUMG + j, e : 2 * P : E],
                                rhs=ones[:, 0:1],
                                start=(j == 0),
                                stop=(j == SUMG - 1),
                            )
                if q == 3:
                    wt_ps = pss.tile([P, T, O], BF16, tag="setup")
                    for t in range(T):
                        for h in range(2):
                            nc.tensor.transpose(
                                wt_ps[:, t, h * P : (h + 1) * P],
                                w_sb[:, h, t:K:T],
                                ident[:],
                            )
                    nc.tensor.matmul(out=b2_ps, lhsT=ones[:], rhs=b2z[:], start=True, stop=True)

            nc.vector.tensor_reduce(
                out=sxs[:], in_=sx_ps.rearrange("p (k e) -> p e k", e=E), axis=AX.X, op=ALU.add
            )
            for h in range(2):
                nc.scalar.copy(out=b2b[:, h, :], in_=b2_ps)
            nc.vector.bn_aggr(out=agg[:, 0, :], in_=st[:, :, 0, :])
            nc.vector.bn_aggr(out=agg[:, 1, :], in_=st[:, :, 1, :])
            nc.vector.scalar_tensor_tensor(
                out=dm[:], in0=sxs[:], scalar=1.0 / B, in1=negm0[:], op0=ALU.mult, op1=ALU.add
            )
            nc.vector.tensor_copy(out=mv[:, 1], in_=agg[:].rearrange("p e s -> p s e"))
            nc.vector.tensor_tensor(out=dm2[:], in0=dm[:], in1=dm[:], op=ALU.mult)
            nc.vector.tensor_reduce(
                out=sqs[:], in_=sq[:].rearrange("p (e q) -> p e q", q=NU), axis=AX.X, op=ALU.add
            )
            nc.vector.tensor_tensor(out=mv[:, 0, 0, :], in0=dm[:], in1=negm0[:], op=ALU.subtract)
            nc.vector.scalar_tensor_tensor(
                out=mv[:, 0, 1, :], in0=sqs[:], scalar=1.0 / B, in1=dm2[:], op0=ALU.mult, op1=ALU.subtract
            )
            nc.vector.tensor_copy(out=wt_sb[:], in_=wt_ps[:])
            nc.gpsimd.tensor_copy(out=wg[:], in_=wt_sb[:].rearrange("p t o -> p o t"))
            transpose_chunks([0, 1], range(T - 1))
            rels = []
            for v in range(U):
                rel = pst.tile([P, UC], F32, tag="tp", name="rel")
                rels.append(rel)
            for u in (1, 0):
                for v in range(U):
                    c0 = P + v - P * u
                    nc.tensor.matmul(
                        out=rels[v][:, 0 : 2 * E],
                        lhsT=J[:, c0 : c0 + 2 * P - 1 : 2],
                        rhs=mv[:, u].rearrange("p s e -> p (s e)"),
                        start=(u == 1),
                        stop=(u == 0),
                    )
            transpose_chunks([0, 1], range(T - 1, T))
            for v in range(U):
                f = slice(v * E, (v + 1) * E)
                nc.scalar.activation(
                    out=std[:, f], in_=rels[v][:, E : 2 * E], func=ACT.Sqrt, bias=eps[:, 0:1]
                )
            nc.scalar.activation(out=warm[:], in_=one1[:], func=ACT.Abs_reciprocal_sqrt)
            for v in range(U):
                f = slice(v * E, (v + 1) * E)
                nc.vector.scalar_tensor_tensor(
                    out=nmg[:, f], in0=rels[v][:, 0:E], scalar=-1.0, in1=gbT[:, f], op0=ALU.mult, op1=ALU.mult
                )
            nc.vector.reciprocal(out=rstd[:], in_=std[:])

        zpool = ctx.enter_context(tc.tile_pool(name="zpool", bufs=2))
        gpool = ctx.enter_context(tc.tile_pool(name="gpool", bufs=3))
        qpool = ctx.enter_context(tc.tile_pool(name="qpool", bufs=3))
        ppool = ctx.enter_context(tc.tile_pool(name="ppool", bufs=5))
        spool = ctx.enter_context(tc.tile_pool(name="spool", bufs=5))
        kpool = ctx.enter_context(tc.tile_pool(name="kpool", bufs=2))
        psm = ctx.enter_context(tc.psum_pool(name="psm", bufs=CMAX // 2))
        def affine(c):
            n = CHUNKS[c] * P
            Zs[c] = zpool.tile([P, T, CMAX * P], BF16, tag="Z", name="Z")
            for t in range(T):
                if c in (0, 2) and t >= T // 2:
                    nc.scalar.activation(
                        out=Zs[c][:, t, 0:n],
                        in_=Xs[c][t][:, 0:n],
                        func=ACT.Identity,
                        scale=sc[:, t : t + 1],
                        bias=sh[:, t : t + 1],
                    )
                    continue
                nc.vector.tensor_scalar(
                    out=Zs[c][:, t, 0:n],
                    in0=Xs[c][t][:, 0:n],
                    scalar1=sc[:, t : t + 1],
                    scalar2=sh[:, t : t + 1],
                    op0=ALU.mult,
                    op1=ALU.add,
                )

        def regroup(c):
            n = CHUNKS[c] * P
            cv = n // 2 if c < 2 or c >= NCH - 3 else n // 4
            Gs[c] = gpool.tile([P, CMAX * P, T], BF16, tag="Gt", name="Gt", align_bytes=64)
            nc.vector.tensor_scalar(
                out=Gs[c][:, 0:cv, :].rearrange("p (c i) t -> p c t i", i=4),
                in0=Zs[c][:, :, 0:cv].rearrange("p t (c i) -> p c t i", i=4),
                scalar1=0.0,
                scalar2=None,
                op0=ALU.max,
            )
            nc.scalar.activation(
                out=Gs[c][:, cv:n, :].rearrange("p (c i) t -> p c t i", i=4),
                in_=Zs[c][:, :, cv:n].rearrange("p t (c i) -> p c t i", i=4),
                func=ACT.Relu,
            )

        def quantise_multiply(c):
            n = CHUNKS[c] * P
            Cs[c] = qpool.tile([P, CMAX * P], U32, tag="codes", name="codes", align_bytes=64)
            Ss[c] = qpool.tile([P, CMAX * P], U8, tag="scales", name="scales", align_bytes=64)
            nc.vector.quantize_mx(
                out=Cs[c][:, 0:n].bitcast(FP8X4),
                scales=Ss[c][:, 0:n],
                in_=Gs[c][:, 0:n, :].rearrange("p b t -> p (b t)"),
            )
            As[c] = []
            for i in range(CHUNKS[c] // 2):
                acc = psm.tile([P, 2, O], F32, tag="acc", name="acc")
                As[c].append(acc)
                for h in range(2):
                    m = slice((2 * i + h) * P, (2 * i + h + 1) * P)
                    nc.tensor.matmul_mx(
                        out=acc[:, h, :],
                        lhsT=Cs[c][:, m].bitcast(FP8X4),
                        lhsT_scale=Ss[c][:, m],
                        rhs=w_codes[:].bitcast(FP8X4),
                        rhs_scale=w_scales[:],
                        start=True,
                        stop=True,
                    )

        def bias_squares(c):
            ng = CHUNKS[c]
            Ps[c] = ppool.tile([P, CMAX, O], F32, tag="Pt", name="Pt")
            ss = spool.tile([P, CMAX], F32, tag="ss")
            for i in range(ng // 2):
                nc.vector.tensor_tensor(
                    out=Ps[c][:, 2 * i : 2 * i + 2, :], in0=As[c][i][:], in1=b2b[:], op=ALU.add
                )
            for r in range(ng):
                if c == NCH - 1 and r % 2:
                    junk3 = kpool.tile([P, O], F32, tag="junk3")
                    nc.vector.scalar_tensor_tensor(
                        out=junk3[:],
                        in0=Ps[c][:, r, :],
                        scalar=1.0,
                        in1=Ps[c][:, r, :],
                        op0=ALU.mult,
                        op1=ALU.mult,
                        accum_out=ss[:, r : r + 1],
                    )
                    continue
                junk2 = kpool.tile([P, O], BF16, tag="junk2")
                nc.scalar.activation(
                    out=junk2[:], in_=Ps[c][:, r, :], func=ACT.Square, accum_out=ss[:, r : r + 1]
                )
            Ns[c] = ss

        def invert_norm(c):
            ng = CHUNKS[c]
            RIs[c] = spool.tile([P, CMAX], F32, tag="rinv", name="rinv")
            nc.scalar.activation(
                out=RIs[c][:, 0:ng], in_=Ns[c][:, 0:ng], func=ACT.Abs_reciprocal_sqrt, bias=tiny[:, 0:1]
            )

        def clamp_norm(c):
            ng = CHUNKS[c]
            rc = spool.tile([P, CMAX], F32, tag="rclamp", name="rc")
            nc.vector.tensor_scalar(
                out=rc[:, 0:ng], in0=RIs[c][:, 0:ng], scalar1=1.0 / L2_EPS, scalar2=None, op0=ALU.min
            )
            RIs[c] = rc

        def shares(c):
            ng = CHUNKS[c]
            if c >= NCH - 2:
                return 0, ng // 2
            if c >= NCH - 4:
                return ng // 2, ng // 4
            return 7 * ng // 8, ng - 7 * ng // 8

        def scale_gpsimd(c):
            for r in range(shares(c)[0]):
                nc.gpsimd.tensor_scalar(
                    out=Ps[c][:, r, :],
                    in0=Ps[c][:, r, :],
                    scalar1=RIs[c][:, r : r + 1],
                    scalar2=1.0,
                    op0=ALU.mult,
                    op1=ALU.mult,
                )

        def scale_store(c):
            ng = CHUNKS[c]
            gp, vec = shares(c)
            for r in range(gp, ng):
                if r < gp + vec:
                    nc.vector.tensor_scalar(
                        out=Ps[c][:, r, :],
                        in0=Ps[c][:, r, :],
                        scalar1=RIs[c][:, r : r + 1],
                        scalar2=None,
                        op0=ALU.mult,
                    )
                else:
                    nc.scalar.activation(
                        out=Ps[c][:, r, :], in_=Ps[c][:, r, :], func=ACT.Copy, scale=RIs[c][:, r : r + 1]
                    )
            cuts = [0, ng] if c < NCH - 4 or gp == 0 else [gp, ng, 0, gp]
            for k in range(0, len(cuts), 2):
                r0, r1 = cuts[k], cuts[k + 1]
                nc.sync.dma_start(
                    out=ov[:, starts[c] + r0 : starts[c] + r1, :], in_=Ps[c][:, r0:r1, :]
                )

        nc.vector.tensor_tensor(out=nms[:], in0=nmg[:], in1=rstd[:], op=ALU.mult)
        nc.vector.tensor_tensor(out=sc[:], in0=gbT[:, 0:T], in1=rstd[:], op=ALU.mult)
        nc.vector.tensor_tensor(out=sh[:], in0=nms[:], in1=gbT[:, T : 2 * T], op=ALU.add)
        affine(0)
        for i in range(NCH + 2):
            if 0 <= i - 2:
                clamp_norm(i - 2)
                scale_gpsimd(i - 2)
            if i + 1 < NCH:
                affine(i + 1)
            if i + 2 < NCH:
                transpose_chunks([i + 2])
            if 0 <= i - 1 < NCH:
                bias_squares(i - 1)
            if i == 0:
                regroup(0)
                nc.vector.quantize_mx(
                    out=w_codes[:].bitcast(FP8X4),
                    scales=w_scales[:],
                    in_=wg[:].rearrange("p o t -> p (o t)"),
                )
            if NCH - 3 <= i - 1 < NCH:
                invert_norm(i - 1)
            if 0 <= i - 2:
                scale_store(i - 2)
            if 0 <= i - 1 < NCH - 3:
                invert_norm(i - 1)
            if i < NCH:
                quantise_multiply(i)
            if i + 1 < NCH:
                regroup(i + 1)
